import numpy as np
import ml_dtypes


def mxq(x, axis, fmt="e4m3"):
    dtype, down = {"e4m3": (ml_dtypes.float8_e4m3fn, 7), "e5m2": (ml_dtypes.float8_e5m2, 14)}[fmt]
    v = np.moveaxis(np.asarray(x, np.float32).astype(ml_dtypes.bfloat16).astype(np.float64), axis, -1)
    blocks = v.reshape(v.shape[:-1] + (-1, 32))
    amax = np.abs(blocks).max(-1, keepdims=True)
    byte = np.maximum(np.where(amax > 0, np.frexp(amax)[1] - 1 + 127, 0) - down, 1)
    scale = np.exp2(byte - 127.0)
    codes = (blocks / scale).astype(np.float32).astype(dtype).astype(np.float64)
    return np.moveaxis((codes * scale).reshape(v.shape), -1, axis)


WIDE = False


def mx_kscale(k):
    if not WIDE:
        return np.ones(k)
    levels = np.array([10, -10, 5, -5, 0])
    a = np.random.permutation(np.resize(levels, k // 512 * 4)).reshape(k // 512, 4)
    idx = np.arange(k)
    return np.exp2(a[idx // 512, idx % 128 // 32])


BF16 = ml_dtypes.bfloat16


def bf(x):
    return np.asarray(x, np.float32).astype(BF16)


def f64(x):
    return np.asarray(x).astype(np.float64)


E2M1 = np.array([0.0, 0.5, 1.0, 1.5, 2.0, 3.0, 4.0, 6.0, -0.0, -0.5, -1.0, -1.5, -2.0, -3.0, -4.0, -6.0])


def pack_weight(w, fmt):
    k, n = w.shape
    w = f64(bf(w)).reshape(k // 32, 32, n)
    amax = np.abs(w).max(1)
    if fmt == "e4m3":
        byte = np.frexp(amax)[1] - 1 + 127 - 7
    else:
        mant, ex = np.frexp(amax / 6.0)
        byte = np.where(mant > 0.5, ex, ex - 1) + 127
    byte = np.clip(np.where(amax > 0, byte, 1), 1, 254)
    scaled = (w * np.exp2(127.0 - byte)[:, None, :]).reshape(k, n).astype(np.float32)
    by_word = np.ascontiguousarray(scaled.reshape(k // 512, 128, 4, n).transpose(0, 1, 3, 2))
    if fmt == "e4m3":
        words = by_word.astype(ml_dtypes.float8_e4m3fn).view(np.uint8)
    else:
        c = by_word.astype(ml_dtypes.float4_e2m1fn).view(np.uint8) & 0xF
        words = c[..., 0::2] | (c[..., 1::2] << 4)
    return np.ascontiguousarray(words), np.ascontiguousarray(byte.astype(np.uint8).reshape(k // 512, 16, n))


def unpack_weight(words, scales, fmt):
    g, p, n, _ = words.shape
    if fmt == "e4m3":
        vals = np.ascontiguousarray(words).view(ml_dtypes.float8_e4m3fn).astype(np.float64)
    else:
        nib = np.empty((g, p, n, 4), np.uint8)
        nib[..., 0::2] = words & 0xF
        nib[..., 1::2] = words >> 4
        vals = E2M1[nib]
    vals = vals * np.repeat(np.exp2(scales.astype(np.float64) - 127.0), 8, axis=1)[..., None]
    return vals.transpose(0, 1, 3, 2).reshape(g * 512, n)

def pack4(w):
    words, scales = pack_weight(w, "e2m1")
    return words.reshape(words.shape[0], 128, -1), scales


def unpack4(words, scales):
    return unpack_weight(words.reshape(words.shape[0], 128, -1, 2), scales, "e2m1")


B, N, D, DO, H, HID = 4, 128, 1024, 128, 8, 2048


def setup_inputs():
    s, t = mx_kscale(D), mx_kscale(D)
    adj = np.random.uniform(size=(N, N))
    adj = adj / adj.sum(-1, keepdims=True)
    h_norm = bf(np.random.standard_normal((B, N, D)) * s)
    o_attn = bf(np.random.standard_normal((B, N, D)) * 0.25 * t)
    a_gcn = bf(adj + np.random.standard_normal((N, N)) * 0.5 / np.sqrt(N))
    w_proj_words, w_proj_scales = pack4(np.random.standard_normal((D, DO)) * 2.0 / np.sqrt(D) / t[:, None])
    b_proj = bf(np.random.standard_normal(DO) * 0.1)
    gcn_w_words, gcn_w_scales = pack4(np.random.standard_normal((D, DO)) / np.sqrt(D) / s[:, None])
    gcn_m = bf(1.0 + 0.1 * np.random.standard_normal(DO))
    return {
        "h_norm": h_norm,
        "o_attn": o_attn,
        "a_gcn": a_gcn,
        "w_proj_words": w_proj_words,
        "w_proj_scales": w_proj_scales,
        "b_proj": b_proj,
        "gcn_w_words": gcn_w_words,
        "gcn_w_scales": gcn_w_scales,
        "gcn_m": gcn_m,
    }


def reference(h_norm, o_attn, a_gcn, w_proj_words, w_proj_scales, b_proj, gcn_w_words, gcn_w_scales, gcn_m):
    o = (mxq(f64(o_attn), 2, "e4m3") @ unpack4(w_proj_words, w_proj_scales)) + f64(b_proj)
    agg = f64(a_gcn) @ f64(h_norm)
    g = (mxq(agg, 2, "e4m3") @ unpack4(gcn_w_words, gcn_w_scales)) * f64(gcn_m)
    return o + g

@@ -1,0 +1,167 @@
+from contextlib import ExitStack
+
+import concourse.mybir as mybir
+from concourse.masks import make_identity
+
+BF16 = mybir.dt.bfloat16
+F32 = mybir.dt.float32
+I32 = mybir.dt.int32
+U32 = mybir.dt.uint32
+U8 = mybir.dt.uint8
+FP8X4 = mybir.dt.float8_e4m3fn_x4
+FP4X4 = mybir.dt.float4_e2m1fn_x4
+MULT = mybir.AluOpType.mult
+ADD = mybir.AluOpType.add
+
+P = 128
+SAMPLES = 4
+NODES = 128
+FEATURES = 1024
+OUT_FEATURES = 128
+PACK = 4
+K_PASS = P * PACK
+PASSES = FEATURES // K_PASS
+PAIRS = PACK // 2
+QUADRANTS = 4
+LIVE_ROWS = 4
+
+FEATURE_BANKS = 5
+ATTENTION_PRODUCT_BANKS = 2
+
+FLOPS = 2 * (2 * SAMPLES * NODES * FEATURES * OUT_FEATURES) + 2 * SAMPLES * NODES * NODES * FEATURES
+
+
+def tile_gatblock_pa_s_kernel(
+    tc, h_norm, o_attn, a_gcn, w_proj_words, w_proj_scales, b_proj, gcn_w_words, gcn_w_scales, gcn_m, out
+):
+    nc = tc.nc
+    with ExitStack() as ctx:
+        const = ctx.enter_context(tc.tile_pool(name="const", bufs=1))
+        per_sample = ctx.enter_context(tc.tile_pool(name="per_sample", bufs=SAMPLES))
+        psum = ctx.enter_context(tc.psum_pool(name="psum", bufs=1))
+
+        ident_bf16 = const.tile([P, P], BF16, name="ident_bf16")
+        make_identity(nc, ident_bf16[:])
+        ident_f32 = const.tile([P, P], F32, name="ident_f32")
+        make_identity(nc, ident_f32[:])
+        ones = const.tile([P, P], BF16, name="ones")
+        nc.vector.memset(ones[:], 1.0)
+        vector_rows = const.tile([P, 2, OUT_FEATURES], BF16, name="vector_rows")
+        nc.vector.memset(vector_rows[:], 0.0)
+
+        def weight_tiles(label):
+            words = const.tile([P, PASSES, 2 * OUT_FEATURES], U8, name="%s_words" % label, align_bytes=64)
+            planes = const.tile([P, PASSES, OUT_FEATURES], U8, name="%s_planes" % label, align_bytes=64)
+            nc.vector.memset(planes[:].bitcast(I32), 0)
+            return words, planes
+
+        def load_weight(words, planes, dram_words, dram_scales):
+            nc.sync.dma_start(out=words[:].bitcast(I32), in_=dram_words.rearrange("g p c -> p g c").bitcast(I32))
+            for quadrant in range(QUADRANTS):
+                nc.sync.dma_start(
+                    out=planes[32 * quadrant : 32 * quadrant + LIVE_ROWS].bitcast(I32),
+                    in_=dram_scales[:, LIVE_ROWS * quadrant : LIVE_ROWS * (quadrant + 1), :]
+                    .rearrange("g r n -> r g n")
+                    .bitcast(I32),
+                )
+
+        gcn_words, gcn_planes = weight_tiles("gcn")
+        proj_words, proj_planes = weight_tiles("proj")
+
+        a_sb = const.tile([P, NODES], BF16, name="a_sb")
+        nc.sync.dma_start(out=a_sb[:], in_=a_gcn)
+        h_sb = []
+        for b in range(SAMPLES):
+            h_tile = per_sample.tile([P, FEATURES], BF16, name="h_sb")
+            nc.sync.dma_start(out=h_tile[:], in_=h_norm[b])
+            h_sb.append(h_tile)
+        load_weight(gcn_words, gcn_planes, gcn_w_words, gcn_w_scales)
+        o_sb = []
+        for b in range(SAMPLES):
+            o_tile = per_sample.tile([P, FEATURES], BF16, name="o_sb")
+            nc.sync.dma_start(out=o_tile[:], in_=o_attn[b])
+            o_sb.append(o_tile)
+        load_weight(proj_words, proj_planes, w_proj_words, w_proj_scales)
+        nc.gpsimd.dma_start(out=vector_rows[0:1, 0, :], in_=b_proj.unsqueeze(0))
+        nc.gpsimd.dma_start(out=vector_rows[0:1, 1, :], in_=gcn_m.unsqueeze(0))
+
+        def copy_out_of_psum(g, dst, src):
+            if g % 2 == 0:
+                nc.vector.tensor_copy(out=dst, in_=src)
+            else:
+                nc.scalar.copy(out=dst, in_=src)
+
+        def quantise(grouped, label):
+            words = per_sample.tile([P, PASSES, NODES], U32, name="%s_words" % label, align_bytes=64)
+            planes = per_sample.tile([P, PASSES, NODES], U8, name="%s_planes" % label, align_bytes=64)
+            nc.vector.quantize_mx(
+                out=words[:].rearrange("p g n -> p (g n)").bitcast(FP8X4),
+                scales=planes[:].rearrange("p g n -> p (g n)"),
+                in_=grouped[:].rearrange("p g n t -> p (g n t)"),
+            )
+            return words, planes
+
+        def multiply_by_weight(product, x_words, x_planes, w_words, w_planes):
+            for g in range(PASSES):
+                nc.tensor.matmul_mx(
+                    out=product,
+                    lhsT=x_words[:, g, :].bitcast(FP8X4),
+                    lhsT_scale=x_planes[:, g, :],
+                    rhs=w_words[:, g, :].bitcast(FP4X4),
+                    rhs_scale=w_planes[:, g, :],
+                    start=(g == 0),
+                    stop=(g == PASSES - 1),
+                )
+
+        a_t_bank = psum.tile([P, NODES], BF16, name="a_t_bank", tag="features", bufs=FEATURE_BANKS)
+        nc.tensor.transpose(a_t_bank[:], a_sb[:], ident_bf16[:])
+        a_t = const.tile([P, NODES], BF16, name="a_t")
+        nc.vector.tensor_copy(out=a_t[:], in_=a_t_bank[:])
+
+        gcn_product = psum.tile([P, SAMPLES, OUT_FEATURES], F32, name="gcn_product")
+        for b in range(SAMPLES):
+            agg_grouped = per_sample.tile([P, PASSES, NODES, PACK], BF16, name="agg_grouped", align_bytes=64)
+            for g in range(PASSES):
+                agg_bank = psum.tile([P, PACK, NODES], F32, name="agg_bank", tag="features", bufs=FEATURE_BANKS)
+                for t in range(PACK):
+                    nc.tensor.matmul(
+                        out=agg_bank[:, t, :],
+                        lhsT=h_sb[b][:, K_PASS * g + t : K_PASS * (g + 1) : PACK],
+                        rhs=a_t[:],
+                        start=True,
+                        stop=True,
+                    )
+                copy_out_of_psum(g, agg_grouped[:, g], agg_bank[:].rearrange("p t n -> p n t"))
+            agg_words, agg_planes = quantise(agg_grouped, "agg")
+            multiply_by_weight(gcn_product[:, b, :], agg_words, agg_planes, gcn_words, gcn_planes)
+
+        spread_bank = psum.tile([P, 2, OUT_FEATURES], F32, name="spread_bank", tag="features", bufs=FEATURE_BANKS)
+        nc.tensor.matmul(out=spread_bank[:], lhsT=ones[:], rhs=vector_rows[:], start=True, stop=True)
+        spread = const.tile([P, 2, OUT_FEATURES], F32, name="spread")
+        nc.scalar.copy(out=spread[:], in_=spread_bank[:])
+        all_samples = [P, SAMPLES, OUT_FEATURES]
+        bias = spread[:, 0, :].unsqueeze(1).to_broadcast(all_samples)
+        gain = spread[:, 1, :].unsqueeze(1).to_broadcast(all_samples)
+
+        gcn_part = const.tile(all_samples, F32, name="gcn_part")
+        nc.vector.tensor_tensor(out=gcn_part[:], in0=gcn_product[:], in1=gain, op=MULT)
+        nc.vector.tensor_tensor(out=gcn_part[:], in0=gcn_part[:], in1=bias, op=ADD)
+
+        for b in range(SAMPLES):
+            att_grouped = per_sample.tile([P, PASSES, NODES, PACK], BF16, name="att_grouped", align_bytes=64)
+            o_pairs = o_sb[b][:].bitcast(F32)
+            for g in range(PASSES):
+                att_bank = psum.tile([P, PAIRS, NODES], F32, name="att_bank", tag="features", bufs=FEATURE_BANKS)
+                for u in range(PAIRS):
+                    nc.tensor.transpose(
+                        att_bank[:, u, :],
+                        o_pairs[:, (K_PASS // 2) * g + u : (K_PASS // 2) * (g + 1) : PAIRS],
+                        ident_f32[:],
+                    )
+                copy_out_of_psum(g, att_grouped[:, g].bitcast(F32), att_bank[:].rearrange("p u n -> p n u"))
+            att_words, att_planes = quantise(att_grouped, "att")
+            att_product = psum.tile([P, OUT_FEATURES], F32, name="att_product", bufs=ATTENTION_PRODUCT_BANKS)
+            multiply_by_weight(att_product[:], att_words, att_planes, proj_words, proj_planes)
+            result = per_sample.tile([P, OUT_FEATURES], F32, name="result")
+            nc.vector.tensor_tensor(out=result[:], in0=att_product[:], in1=gcn_part[:, b, :], op=ADD)
+            nc.sync.dma_start(out=out[b], in_=result[:])

@@ -25,8 +25,10 @@ PAIRS = PACK // 2
 QUADRANTS = 4
 LIVE_ROWS = 4
 
-FEATURE_BANKS = 5
-ATTENTION_PRODUCT_BANKS = 2
+AGG_BANKS = 3
+ATT_BANKS = 2
+GCN_PRODUCT_BANKS = 1
+ATT_PRODUCT_BANKS = 2
 
 FLOPS = 2 * (2 * SAMPLES * NODES * FEATURES * OUT_FEATURES) + 2 * SAMPLES * NODES * NODES * FEATURES
 
@@ -36,18 +38,19 @@ def tile_gatblock_pa_s_kernel(
 ):
     nc = tc.nc
     with ExitStack() as ctx:
+        ctx.enter_context(tc.manual_schedule())
         const = ctx.enter_context(tc.tile_pool(name="const", bufs=1))
         per_sample = ctx.enter_context(tc.tile_pool(name="per_sample", bufs=SAMPLES))
         psum = ctx.enter_context(tc.psum_pool(name="psum", bufs=1))
 
-        ident_bf16 = const.tile([P, P], BF16, name="ident_bf16")
-        make_identity(nc, ident_bf16[:])
         ident_f32 = const.tile([P, P], F32, name="ident_f32")
         make_identity(nc, ident_f32[:])
         ones = const.tile([P, P], BF16, name="ones")
         nc.vector.memset(ones[:], 1.0)
         vector_rows = const.tile([P, 2, OUT_FEATURES], BF16, name="vector_rows")
         nc.vector.memset(vector_rows[:], 0.0)
+        nc.gpsimd.dma_start(out=vector_rows[0:1, 0, :], in_=b_proj.unsqueeze(0))
+        nc.gpsimd.dma_start(out=vector_rows[0:1, 1, :], in_=gcn_m.unsqueeze(0))
 
         def weight_tiles(label):
             words = const.tile([P, PASSES, 2 * OUT_FEATURES], U8, name="%s_words" % label, align_bytes=64)
@@ -65,31 +68,69 @@ def tile_gatblock_pa_s_kernel(
                     .bitcast(I32),
                 )
 
+        def load_sample(dram, b, label):
+            x_sb = per_sample.tile([P, FEATURES], BF16, name=label)
+            nc.sync.dma_start(out=x_sb[:], in_=dram[b])
+            return x_sb
+
         gcn_words, gcn_planes = weight_tiles("gcn")
         proj_words, proj_planes = weight_tiles("proj")
+        ident_bf16 = const.tile([P, P], BF16, name="ident_bf16")
+        nc.vector.tensor_copy(out=ident_bf16[:], in_=ident_f32[:])
 
         a_sb = const.tile([P, NODES], BF16, name="a_sb")
         nc.sync.dma_start(out=a_sb[:], in_=a_gcn)
-        h_sb = []
-        for b in range(SAMPLES):
-            h_tile = per_sample.tile([P, FEATURES], BF16, name="h_sb")
-            nc.sync.dma_start(out=h_tile[:], in_=h_norm[b])
-            h_sb.append(h_tile)
+        h_sb = [load_sample(h_norm, 0, "h_sb")]
         load_weight(gcn_words, gcn_planes, gcn_w_words, gcn_w_scales)
-        o_sb = []
-        for b in range(SAMPLES):
-            o_tile = per_sample.tile([P, FEATURES], BF16, name="o_sb")
-            nc.sync.dma_start(out=o_tile[:], in_=o_attn[b])
-            o_sb.append(o_tile)
+        h_sb.append(load_sample(h_norm, 1, "h_sb"))
+        o_sb = [load_sample(o_attn, 0, "o_sb")]
         load_weight(proj_words, proj_planes, w_proj_words, w_proj_scales)
-        nc.gpsimd.dma_start(out=vector_rows[0:1, 0, :], in_=b_proj.unsqueeze(0))
-        nc.gpsimd.dma_start(out=vector_rows[0:1, 1, :], in_=gcn_m.unsqueeze(0))
+        for b in range(2, SAMPLES):
+            h_sb.append(load_sample(h_norm, b, "h_sb"))
+            o_sb.append(load_sample(o_attn, b - 1, "o_sb"))
+        o_sb.append(load_sample(o_attn, SAMPLES - 1, "o_sb"))
 
-        def copy_out_of_psum(g, dst, src):
-            if g % 2 == 0:
-                nc.vector.tensor_copy(out=dst, in_=src)
-            else:
-                nc.scalar.copy(out=dst, in_=src)
+        a_t_bank = psum.tile([P, NODES], BF16, name="a_t_bank", tag="att_bank", bufs=ATT_BANKS)
+        nc.tensor.transpose(a_t_bank[:], a_sb[:], ident_bf16[:])
+        a_t = const.tile([P, NODES], BF16, name="a_t")
+        nc.vector.tensor_copy(out=a_t[:], in_=a_t_bank[:])
+
+        agg_grouped, agg_mx, att_grouped, att_mx, gcn_product, gcn_part, att_product = {}, {}, {}, {}, {}, {}, {}
+
+        def grouped_tile(label):
+            return per_sample.tile([P, PASSES, NODES, PACK], BF16, name=label, align_bytes=64)
+
+        def aggregate(b):
+            agg_grouped[b] = grouped_tile("agg_grouped")
+            for g in range(PASSES):
+                agg_bank = psum.tile([P, PACK, NODES], F32, name="agg_bank", bufs=AGG_BANKS)
+                for t in range(PACK):
+                    nc.tensor.matmul(
+                        out=agg_bank[:, t, :],
+                        lhsT=h_sb[b][:, K_PASS * g + t : K_PASS * (g + 1) : PACK],
+                        rhs=a_t[:],
+                        start=True,
+                        stop=True,
+                    )
+                nc.scalar.copy(out=agg_grouped[b][:, g], in_=agg_bank[:].rearrange("p t n -> p n t"))
+
+        def transpose_attention(b):
+            att_grouped[b] = grouped_tile("att_grouped")
+            o_pairs = o_sb[b][:].bitcast(F32)
+            for g in range(PASSES):
+                att_bank = psum.tile([P, PAIRS, NODES], F32, name="att_bank", bufs=ATT_BANKS)
+                for u in range(PAIRS):
+                    nc.tensor.transpose(
+                        att_bank[:, u, :],
+                        o_pairs[:, (K_PASS // 2) * g + u : (K_PASS // 2) * (g + 1) : PAIRS],
+                        ident_f32[:],
+                    )
+                dst = att_grouped[b][:, g].bitcast(F32)
+                src = att_bank[:].rearrange("p u n -> p n u")
+                if g % 2 == 0:
+                    nc.vector.tensor_copy(out=dst, in_=src)
+                else:
+                    nc.scalar.copy(out=dst, in_=src)
 
         def quantise(grouped, label):
             words = per_sample.tile([P, PASSES, NODES], U32, name="%s_words" % label, align_bytes=64)
@@ -101,10 +142,12 @@ def tile_gatblock_pa_s_kernel(
             )
             return words, planes
 
-        def multiply_by_weight(product, x_words, x_planes, w_words, w_planes):
+        def multiply_by_weight(label, banks, x_mx, w_words, w_planes):
+            product = psum.tile([P, OUT_FEATURES], F32, name=label, bufs=banks)
+            x_words, x_planes = x_mx
             for g in range(PASSES):
                 nc.tensor.matmul_mx(
-                    out=product,
+                    out=product[:],
                     lhsT=x_words[:, g, :].bitcast(FP8X4),
                     lhsT_scale=x_planes[:, g, :],
                     rhs=w_words[:, g, :].bitcast(FP4X4),
@@ -112,56 +155,44 @@ def tile_gatblock_pa_s_kernel(
                     start=(g == 0),
                     stop=(g == PASSES - 1),
                 )
+            return product
 
-        a_t_bank = psum.tile([P, NODES], BF16, name="a_t_bank", tag="features", bufs=FEATURE_BANKS)
-        nc.tensor.transpose(a_t_bank[:], a_sb[:], ident_bf16[:])
-        a_t = const.tile([P, NODES], BF16, name="a_t")
-        nc.vector.tensor_copy(out=a_t[:], in_=a_t_bank[:])
+        def scale_gcn_product(b):
+            scaled = per_sample.tile([P, OUT_FEATURES], F32, name="scaled")
+            nc.vector.tensor_tensor(out=scaled[:], in0=gcn_product[b][:], in1=spread[:, 1, :], op=MULT)
+            gcn_part[b] = per_sample.tile([P, OUT_FEATURES], F32, name="gcn_part")
+            nc.gpsimd.tensor_tensor(out=gcn_part[b][:], in0=scaled[:], in1=spread[:, 0, :], op=ADD)
 
-        gcn_product = psum.tile([P, SAMPLES, OUT_FEATURES], F32, name="gcn_product")
-        for b in range(SAMPLES):
-            agg_grouped = per_sample.tile([P, PASSES, NODES, PACK], BF16, name="agg_grouped", align_bytes=64)
-            for g in range(PASSES):
-                agg_bank = psum.tile([P, PACK, NODES], F32, name="agg_bank", tag="features", bufs=FEATURE_BANKS)
-                for t in range(PACK):
-                    nc.tensor.matmul(
-                        out=agg_bank[:, t, :],
-                        lhsT=h_sb[b][:, K_PASS * g + t : K_PASS * (g + 1) : PACK],
-                        rhs=a_t[:],
-                        start=True,
-                        stop=True,
-                    )
-                copy_out_of_psum(g, agg_grouped[:, g], agg_bank[:].rearrange("p t n -> p n t"))
-            agg_words, agg_planes = quantise(agg_grouped, "agg")
-            multiply_by_weight(gcn_product[:, b, :], agg_words, agg_planes, gcn_words, gcn_planes)
-
-        spread_bank = psum.tile([P, 2, OUT_FEATURES], F32, name="spread_bank", tag="features", bufs=FEATURE_BANKS)
-        nc.tensor.matmul(out=spread_bank[:], lhsT=ones[:], rhs=vector_rows[:], start=True, stop=True)
-        spread = const.tile([P, 2, OUT_FEATURES], F32, name="spread")
-        nc.scalar.copy(out=spread[:], in_=spread_bank[:])
-        all_samples = [P, SAMPLES, OUT_FEATURES]
-        bias = spread[:, 0, :].unsqueeze(1).to_broadcast(all_samples)
-        gain = spread[:, 1, :].unsqueeze(1).to_broadcast(all_samples)
-
-        gcn_part = const.tile(all_samples, F32, name="gcn_part")
-        nc.vector.tensor_tensor(out=gcn_part[:], in0=gcn_product[:], in1=gain, op=MULT)
-        nc.vector.tensor_tensor(out=gcn_part[:], in0=gcn_part[:], in1=bias, op=ADD)
-
-        for b in range(SAMPLES):
-            att_grouped = per_sample.tile([P, PASSES, NODES, PACK], BF16, name="att_grouped", align_bytes=64)
-            o_pairs = o_sb[b][:].bitcast(F32)
-            for g in range(PASSES):
-                att_bank = psum.tile([P, PAIRS, NODES], F32, name="att_bank", tag="features", bufs=FEATURE_BANKS)
-                for u in range(PAIRS):
-                    nc.tensor.transpose(
-                        att_bank[:, u, :],
-                        o_pairs[:, (K_PASS // 2) * g + u : (K_PASS // 2) * (g + 1) : PAIRS],
-                        ident_f32[:],
-                    )
-                copy_out_of_psum(g, att_grouped[:, g].bitcast(F32), att_bank[:].rearrange("p u n -> p n u"))
-            att_words, att_planes = quantise(att_grouped, "att")
-            att_product = psum.tile([P, OUT_FEATURES], F32, name="att_product", bufs=ATTENTION_PRODUCT_BANKS)
-            multiply_by_weight(att_product[:], att_words, att_planes, proj_words, proj_planes)
+        def finish(b):
             result = per_sample.tile([P, OUT_FEATURES], F32, name="result")
-            nc.vector.tensor_tensor(out=result[:], in0=att_product[:], in1=gcn_part[:, b, :], op=ADD)
+            nc.vector.tensor_tensor(out=result[:], in0=att_product[b][:], in1=gcn_part[b][:], op=ADD)
             nc.sync.dma_start(out=out[b], in_=result[:])
+
+        def is_sample(b):
+            return 0 <= b < SAMPLES
+
+        spread = const.tile([P, 2, OUT_FEATURES], F32, name="spread")
+        for s in range(SAMPLES + 3):
+            if is_sample(s - 2):
+                scale_gcn_product(s - 2)
+                att_mx[s - 2] = quantise(att_grouped[s - 2], "att")
+            if is_sample(s - 3):
+                finish(s - 3)
+            if is_sample(s):
+                aggregate(s)
+            if is_sample(s - 1):
+                transpose_attention(s - 1)
+            if s == 1:
+                spread_bank = psum.tile([P, 2, OUT_FEATURES], F32, name="spread_bank", tag="att_bank", bufs=ATT_BANKS)
+                nc.tensor.matmul(out=spread_bank[:], lhsT=ones[:], rhs=vector_rows[:], start=True, stop=True)
+                nc.scalar.copy(out=spread[:], in_=spread_bank[:])
+            if is_sample(s):
+                agg_mx[s] = quantise(agg_grouped[s], "agg")
+            if is_sample(s - 1):
+                gcn_product[s - 1] = multiply_by_weight(
+                    "gcn_product", GCN_PRODUCT_BANKS, agg_mx[s - 1], gcn_words, gcn_planes
+                )
+            if is_sample(s - 2):
+                att_product[s - 2] = multiply_by_weight(
+                    "att_product", ATT_PRODUCT_BANKS, att_mx[s - 2], proj_words, proj_planes
+                )

@@ -95,10 +95,18 @@ def tile_gatblock_pa_s_kernel(
         a_t = const.tile([P, NODES], BF16, name="a_t")
         nc.vector.tensor_copy(out=a_t[:], in_=a_t_bank[:])
 
-        agg_grouped, agg_mx, att_grouped, att_mx, gcn_product, gcn_part, att_product = {}, {}, {}, {}, {}, {}, {}
+        h_sorted, agg_grouped, agg_mx, att_grouped, att_mx = {}, {}, {}, {}, {}
+        gcn_product, gcn_part, att_product = {}, {}, {}
 
         def grouped_tile(label):
             return per_sample.tile([P, PASSES, NODES, PACK], BF16, name=label, align_bytes=64)
+
+        def sort_pairs(b):
+            h_sorted[b] = per_sample.tile([P, PASSES, PAIRS, P, 2], BF16, name="h_sorted")
+            nc.vector.tensor_copy(
+                out=h_sorted[b][:].rearrange("m g u p e -> m g u (p e)").bitcast(I32),
+                in_=h_sb[b][:].bitcast(I32).rearrange("m (g p u) -> m g u p", g=PASSES, u=PAIRS),
+            )
 
         def aggregate(b):
             agg_grouped[b] = grouped_tile("agg_grouped")
@@ -107,7 +115,7 @@ def tile_gatblock_pa_s_kernel(
                 for t in range(PACK):
                     nc.tensor.matmul(
                         out=agg_bank[:, t, :],
-                        lhsT=h_sb[b][:, K_PASS * g + t : K_PASS * (g + 1) : PACK],
+                        lhsT=h_sorted[b][:, g, t // 2, :, t % 2],
                         rhs=a_t[:],
                         start=True,
                         stop=True,
@@ -172,12 +180,15 @@ def tile_gatblock_pa_s_kernel(
             return 0 <= b < SAMPLES
 
         spread = const.tile([P, 2, OUT_FEATURES], F32, name="spread")
+        sort_pairs(0)
         for s in range(SAMPLES + 3):
             if is_sample(s - 2):
                 scale_gcn_product(s - 2)
                 att_mx[s - 2] = quantise(att_grouped[s - 2], "att")
             if is_sample(s - 3):
                 finish(s - 3)
+            if is_sample(s + 1):
+                sort_pairs(s + 1)
             if is_sample(s):
                 aggregate(s)
             if is_sample(s - 1):

@@ -95,18 +95,11 @@ def tile_gatblock_pa_s_kernel(
         a_t = const.tile([P, NODES], BF16, name="a_t")
         nc.vector.tensor_copy(out=a_t[:], in_=a_t_bank[:])
 
-        h_sorted, agg_grouped, agg_mx, att_grouped, att_mx = {}, {}, {}, {}, {}
-        gcn_product, gcn_part, att_product = {}, {}, {}
+        agg_grouped, agg_mx, att_grouped, att_mx = {}, {}, {}, {}
+        gcn_product, scaled, gcn_part, att_product = {}, {}, {}, {}
 
         def grouped_tile(label):
             return per_sample.tile([P, PASSES, NODES, PACK], BF16, name=label, align_bytes=64)
-
-        def sort_pairs(b):
-            h_sorted[b] = per_sample.tile([P, PASSES, PAIRS, P, 2], BF16, name="h_sorted")
-            nc.vector.tensor_copy(
-                out=h_sorted[b][:].rearrange("m g u p e -> m g u (p e)").bitcast(I32),
-                in_=h_sb[b][:].bitcast(I32).rearrange("m (g p u) -> m g u p", g=PASSES, u=PAIRS),
-            )
 
         def aggregate(b):
             agg_grouped[b] = grouped_tile("agg_grouped")
@@ -115,7 +108,7 @@ def tile_gatblock_pa_s_kernel(
                 for t in range(PACK):
                     nc.tensor.matmul(
                         out=agg_bank[:, t, :],
-                        lhsT=h_sorted[b][:, g, t // 2, :, t % 2],
+                        lhsT=h_sb[b][:, K_PASS * g + t : K_PASS * (g + 1) : PACK],
                         rhs=a_t[:],
                         start=True,
                         stop=True,
@@ -166,10 +159,12 @@ def tile_gatblock_pa_s_kernel(
             return product
 
         def scale_gcn_product(b):
-            scaled = per_sample.tile([P, OUT_FEATURES], F32, name="scaled")
-            nc.vector.tensor_tensor(out=scaled[:], in0=gcn_product[b][:], in1=spread[:, 1, :], op=MULT)
+            scaled[b] = per_sample.tile([P, OUT_FEATURES], F32, name="scaled")
+            nc.vector.tensor_tensor(out=scaled[b][:], in0=gcn_product[b][:], in1=spread[:, 1, :], op=MULT)
+
+        def add_bias(b):
             gcn_part[b] = per_sample.tile([P, OUT_FEATURES], F32, name="gcn_part")
-            nc.gpsimd.tensor_tensor(out=gcn_part[b][:], in0=scaled[:], in1=spread[:, 0, :], op=ADD)
+            nc.vector.tensor_tensor(out=gcn_part[b][:], in0=scaled[b][:], in1=spread[:, 0, :], op=ADD)
 
         def finish(b):
             result = per_sample.tile([P, OUT_FEATURES], F32, name="result")
@@ -180,15 +175,13 @@ def tile_gatblock_pa_s_kernel(
             return 0 <= b < SAMPLES
 
         spread = const.tile([P, 2, OUT_FEATURES], F32, name="spread")
-        sort_pairs(0)
         for s in range(SAMPLES + 3):
             if is_sample(s - 2):
                 scale_gcn_product(s - 2)
                 att_mx[s - 2] = quantise(att_grouped[s - 2], "att")
+                add_bias(s - 2)
             if is_sample(s - 3):
                 finish(s - 3)
-            if is_sample(s + 1):
-                sort_pairs(s + 1)
             if is_sample(s):
                 aggregate(s)
             if is_sample(s - 1):

@@ -80,15 +80,20 @@ def tile_gatblock_pa_s_kernel(
 
         a_sb = const.tile([P, NODES], BF16, name="a_sb")
         nc.sync.dma_start(out=a_sb[:], in_=a_gcn)
-        h_sb = [load_sample(h_norm, 0, "h_sb")]
+        o_first = per_sample.tile([P, FEATURES], BF16, name="o_sb")
+        for g in range(PASSES):
+            nc.sync.dma_start(
+                out=o_first[:, K_PASS * g : K_PASS * (g + 1)], in_=o_attn[0][:, K_PASS * g : K_PASS * (g + 1)]
+            )
+        o_sb = [o_first]
+        h_sb = [load_sample(h_norm, 0, "h_sb"), load_sample(h_norm, 1, "h_sb")]
         load_weight(gcn_words, gcn_planes, gcn_w_words, gcn_w_scales)
-        h_sb.append(load_sample(h_norm, 1, "h_sb"))
-        o_sb = [load_sample(o_attn, 0, "o_sb")]
+        h_sb.append(load_sample(h_norm, 2, "h_sb"))
         load_weight(proj_words, proj_planes, w_proj_words, w_proj_scales)
-        for b in range(2, SAMPLES):
-            h_sb.append(load_sample(h_norm, b, "h_sb"))
-            o_sb.append(load_sample(o_attn, b - 1, "o_sb"))
-        o_sb.append(load_sample(o_attn, SAMPLES - 1, "o_sb"))
+        o_sb.append(load_sample(o_attn, 1, "o_sb"))
+        h_sb.append(load_sample(h_norm, 3, "h_sb"))
+        o_sb.append(load_sample(o_attn, 2, "o_sb"))
+        o_sb.append(load_sample(o_attn, 3, "o_sb"))
 
         a_t_bank = psum.tile([P, NODES], BF16, name="a_t_bank", tag="att_bank", bufs=ATT_BANKS)
         nc.tensor.transpose(a_t_bank[:], a_sb[:], ident_bf16[:])
@@ -128,7 +133,7 @@ def tile_gatblock_pa_s_kernel(
                     )
                 dst = att_grouped[b][:, g].bitcast(F32)
                 src = att_bank[:].rearrange("p u n -> p n u")
-                if g % 2 == 0:
+                if g % 2 == 0 and b < SAMPLES - 1:
                     nc.vector.tensor_copy(out=dst, in_=src)
                 else:
                     nc.scalar.copy(out=dst, in_=src)
@@ -175,6 +180,7 @@ def tile_gatblock_pa_s_kernel(
             return 0 <= b < SAMPLES
 
         spread = const.tile([P, 2, OUT_FEATURES], F32, name="spread")
+        transpose_attention(0)
         for s in range(SAMPLES + 3):
             if is_sample(s - 2):
                 scale_gcn_product(s - 2)
@@ -184,7 +190,7 @@ def tile_gatblock_pa_s_kernel(
                 finish(s - 3)
             if is_sample(s):
                 aggregate(s)
-            if is_sample(s - 1):
+            if is_sample(s - 1) and s - 1 > 0:
                 transpose_attention(s - 1)
             if s == 1:
                 spread_bank = psum.tile([P, 2, OUT_FEATURES], F32, name="spread_bank", tag="att_bank", bufs=ATT_BANKS)

@@ -15,6 +15,7 @@ ADD = mybir.AluOpType.add
 
 P = 128
 SAMPLES = 4
+LAST = SAMPLES - 1
 NODES = 128
 FEATURES = 1024
 OUT_FEATURES = 128
@@ -138,9 +139,13 @@ def tile_gatblock_pa_s_kernel(
                 else:
                     nc.scalar.copy(out=dst, in_=src)
 
-        def quantise(grouped, label):
+        def mx_tiles(label):
             words = per_sample.tile([P, PASSES, NODES], U32, name="%s_words" % label, align_bytes=64)
             planes = per_sample.tile([P, PASSES, NODES], U8, name="%s_planes" % label, align_bytes=64)
+            return words, planes
+
+        def quantise(grouped, label):
+            words, planes = mx_tiles(label)
             nc.vector.quantize_mx(
                 out=words[:].rearrange("p g n -> p (g n)").bitcast(FP8X4),
                 scales=planes[:].rearrange("p g n -> p (g n)"),
@@ -148,19 +153,30 @@ def tile_gatblock_pa_s_kernel(
             )
             return words, planes
 
+        def quantise_pass(grouped, x_mx, g):
+            words, planes = x_mx
+            nc.vector.quantize_mx(
+                out=words[:, g, :].bitcast(FP8X4),
+                scales=planes[:, g, :],
+                in_=grouped[:, g].rearrange("p n t -> p (n t)"),
+            )
+
+        def multiply_pass(product, x_mx, w_words, w_planes, g):
+            x_words, x_planes = x_mx
+            nc.tensor.matmul_mx(
+                out=product[:],
+                lhsT=x_words[:, g, :].bitcast(FP8X4),
+                lhsT_scale=x_planes[:, g, :],
+                rhs=w_words[:, g, :].bitcast(FP4X4),
+                rhs_scale=w_planes[:, g, :],
+                start=(g == 0),
+                stop=(g == PASSES - 1),
+            )
+
         def multiply_by_weight(label, banks, x_mx, w_words, w_planes):
             product = psum.tile([P, OUT_FEATURES], F32, name=label, bufs=banks)
-            x_words, x_planes = x_mx
             for g in range(PASSES):
-                nc.tensor.matmul_mx(
-                    out=product[:],
-                    lhsT=x_words[:, g, :].bitcast(FP8X4),
-                    lhsT_scale=x_planes[:, g, :],
-                    rhs=w_words[:, g, :].bitcast(FP4X4),
-                    rhs_scale=w_planes[:, g, :],
-                    start=(g == 0),
-                    stop=(g == PASSES - 1),
-                )
+                multiply_pass(product, x_mx, w_words, w_planes, g)
             return product
 
         def scale_gcn_product(b):
@@ -184,7 +200,10 @@ def tile_gatblock_pa_s_kernel(
         for s in range(SAMPLES + 3):
             if is_sample(s - 2):
                 scale_gcn_product(s - 2)
-                att_mx[s - 2] = quantise(att_grouped[s - 2], "att")
+                if s - 2 < LAST:
+                    att_mx[s - 2] = quantise(att_grouped[s - 2], "att")
+                else:
+                    quantise_pass(att_grouped[LAST], att_mx[LAST], 1)
                 add_bias(s - 2)
             if is_sample(s - 3):
                 finish(s - 3)
@@ -192,6 +211,9 @@ def tile_gatblock_pa_s_kernel(
                 aggregate(s)
             if is_sample(s - 1) and s - 1 > 0:
                 transpose_attention(s - 1)
+            if s - 1 == LAST:
+                att_mx[LAST] = mx_tiles("att")
+                quantise_pass(att_grouped[LAST], att_mx[LAST], 0)
             if s == 1:
                 spread_bank = psum.tile([P, 2, OUT_FEATURES], F32, name="spread_bank", tag="att_bank", bufs=ATT_BANKS)
                 nc.tensor.matmul(out=spread_bank[:], lhsT=ones[:], rhs=vector_rows[:], start=True, stop=True)
@@ -202,7 +224,12 @@ def tile_gatblock_pa_s_kernel(
                 gcn_product[s - 1] = multiply_by_weight(
                     "gcn_product", GCN_PRODUCT_BANKS, agg_mx[s - 1], gcn_words, gcn_planes
                 )
-            if is_sample(s - 2):
+            if is_sample(s - 2) and s - 2 < LAST:
                 att_product[s - 2] = multiply_by_weight(
                     "att_product", ATT_PRODUCT_BANKS, att_mx[s - 2], proj_words, proj_planes
                 )
+            if s - 1 == LAST:
+                att_product[LAST] = psum.tile([P, OUT_FEATURES], F32, name="att_product", bufs=ATT_PRODUCT_BANKS)
+                multiply_pass(att_product[LAST], att_mx[LAST], proj_words, proj_planes, 0)
+            if s - 2 == LAST:
+                multiply_pass(att_product[LAST], att_mx[LAST], proj_words, proj_planes, 1)

@@ -197,20 +197,24 @@ def tile_gatblock_pa_s_kernel(
 
         spread = const.tile([P, 2, OUT_FEATURES], F32, name="spread")
         transpose_attention(0)
+        att_mx[0] = quantise(att_grouped[0], "att")
         for s in range(SAMPLES + 3):
             if is_sample(s - 2):
                 scale_gcn_product(s - 2)
-                if s - 2 < LAST:
+                if 0 < s - 2 < LAST:
                     att_mx[s - 2] = quantise(att_grouped[s - 2], "att")
-                else:
+                if s - 2 == LAST:
                     quantise_pass(att_grouped[LAST], att_mx[LAST], 1)
-                add_bias(s - 2)
+                if s - 2 > 0:
+                    add_bias(s - 2)
             if is_sample(s - 3):
                 finish(s - 3)
             if is_sample(s):
                 aggregate(s)
             if is_sample(s - 1) and s - 1 > 0:
                 transpose_attention(s - 1)
+            if s - 2 == 0:
+                add_bias(0)
             if s - 1 == LAST:
                 att_mx[LAST] = mx_tiles("att")
                 quantise_pass(att_grouped[LAST], att_mx[LAST], 0)

@@ -185,7 +185,8 @@ def tile_gatblock_pa_s_kernel(
 
         def add_bias(b):
             gcn_part[b] = per_sample.tile([P, OUT_FEATURES], F32, name="gcn_part")
-            nc.vector.tensor_tensor(out=gcn_part[b][:], in0=scaled[b][:], in1=spread[:, 0, :], op=ADD)
+            engine = nc.vector if b == LAST else nc.gpsimd
+            engine.tensor_tensor(out=gcn_part[b][:], in0=scaled[b][:], in1=spread[:, 0, :], op=ADD)
 
         def finish(b):
             result = per_sample.tile([P, OUT_FEATURES], F32, name="result")

@@ -26,10 +26,11 @@ PAIRS = PACK // 2
 QUADRANTS = 4
 LIVE_ROWS = 4
 
-AGG_BANKS = 3
+AGG_BANKS = 4
 ATT_BANKS = 2
-GCN_PRODUCT_BANKS = 1
-ATT_PRODUCT_BANKS = 2
+PRODUCT_BANKS = 2
+GCN, ATT = 0, 1
+WARM_UPS = 2
 
 FLOPS = 2 * (2 * SAMPLES * NODES * FEATURES * OUT_FEATURES) + 2 * SAMPLES * NODES * NODES * FEATURES
 
@@ -44,14 +45,14 @@ def tile_gatblock_pa_s_kernel(
         per_sample = ctx.enter_context(tc.tile_pool(name="per_sample", bufs=SAMPLES))
         psum = ctx.enter_context(tc.psum_pool(name="psum", bufs=1))
 
+        zeros = const.tile([P, P], F32, name="zeros")
+        nc.vector.memset(zeros[:], 0.0)
         ident_f32 = const.tile([P, P], F32, name="ident_f32")
         make_identity(nc, ident_f32[:])
         ones = const.tile([P, P], BF16, name="ones")
         nc.vector.memset(ones[:], 1.0)
         vector_rows = const.tile([P, 2, OUT_FEATURES], BF16, name="vector_rows")
         nc.vector.memset(vector_rows[:], 0.0)
-        nc.gpsimd.dma_start(out=vector_rows[0:1, 0, :], in_=b_proj.unsqueeze(0))
-        nc.gpsimd.dma_start(out=vector_rows[0:1, 1, :], in_=gcn_m.unsqueeze(0))
 
         def weight_tiles(label):
             words = const.tile([P, PASSES, 2 * OUT_FEATURES], U8, name="%s_words" % label, align_bytes=64)
@@ -80,161 +81,158 @@ def tile_gatblock_pa_s_kernel(
         nc.vector.tensor_copy(out=ident_bf16[:], in_=ident_f32[:])
 
         a_sb = const.tile([P, NODES], BF16, name="a_sb")
+        h_sb = [per_sample.tile([P, FEATURES], BF16, name="h_sb") for b in range(SAMPLES)]
+        o_sb = [per_sample.tile([P, FEATURES], BF16, name="o_sb") for b in range(SAMPLES)]
+
+        def load(tile, dram, first=0, last=FEATURES):
+            nc.sync.dma_start(out=tile[:, first:last], in_=dram[:, first:last])
+
         nc.sync.dma_start(out=a_sb[:], in_=a_gcn)
-        o_first = per_sample.tile([P, FEATURES], BF16, name="o_sb")
-        for g in range(PASSES):
-            nc.sync.dma_start(
-                out=o_first[:, K_PASS * g : K_PASS * (g + 1)], in_=o_attn[0][:, K_PASS * g : K_PASS * (g + 1)]
-            )
-        o_sb = [o_first]
-        h_sb = [load_sample(h_norm, 0, "h_sb"), load_sample(h_norm, 1, "h_sb")]
+        load(o_sb[0], o_attn[0], 0, K_PASS)
+        load(h_sb[0], h_norm[0])
+        load(o_sb[0], o_attn[0], K_PASS, FEATURES)
+        load(h_sb[1], h_norm[1])
+        nc.sync.dma_start(out=vector_rows[0:1, 0, :], in_=b_proj.unsqueeze(0))
+        nc.sync.dma_start(out=vector_rows[0:1, 1, :], in_=gcn_m.unsqueeze(0))
+        load(o_sb[1], o_attn[1])
+        load(h_sb[2], h_norm[2])
+        load(o_sb[2], o_attn[2])
         load_weight(gcn_words, gcn_planes, gcn_w_words, gcn_w_scales)
-        h_sb.append(load_sample(h_norm, 2, "h_sb"))
+        load(h_sb[3], h_norm[3])
+        load(o_sb[3], o_attn[3])
         load_weight(proj_words, proj_planes, w_proj_words, w_proj_scales)
-        o_sb.append(load_sample(o_attn, 1, "o_sb"))
-        h_sb.append(load_sample(h_norm, 3, "h_sb"))
-        o_sb.append(load_sample(o_attn, 2, "o_sb"))
-        o_sb.append(load_sample(o_attn, 3, "o_sb"))
+
+        warm_bank = psum.tile([P, OUT_FEATURES], F32, name="warm_bank", tag="product", bufs=PRODUCT_BANKS)
+        for i in range(WARM_UPS):
+            nc.tensor.matmul(out=warm_bank[:], lhsT=zeros[:], rhs=zeros[:], start=True, stop=True)
 
         a_t_bank = psum.tile([P, NODES], BF16, name="a_t_bank", tag="att_bank", bufs=ATT_BANKS)
         nc.tensor.transpose(a_t_bank[:], a_sb[:], ident_bf16[:])
         a_t = const.tile([P, NODES], BF16, name="a_t")
         nc.vector.tensor_copy(out=a_t[:], in_=a_t_bank[:])
+        spread = const.tile([P, 2, 1, OUT_FEATURES], F32, name="spread")
 
-        agg_grouped, agg_mx, att_grouped, att_mx = {}, {}, {}, {}
-        gcn_product, scaled, gcn_part, att_product = {}, {}, {}, {}
+        grouped, words, planes = [], [], []
+        for b in range(SAMPLES):
+            grouped.append(per_sample.tile([P, 2, PASSES, NODES, PACK], BF16, name="grouped", align_bytes=64))
+            words.append(per_sample.tile([P, 2, PASSES, NODES], U32, name="words", align_bytes=64))
+            planes.append(per_sample.tile([P, 2, PASSES, NODES], U8, name="planes", align_bytes=64))
 
-        def grouped_tile(label):
-            return per_sample.tile([P, PASSES, NODES, PACK], BF16, name=label, align_bytes=64)
+        def aggregate(b, g, copy):
+            agg_bank = psum.tile([P, PACK, NODES], F32, name="agg_bank", bufs=AGG_BANKS)
+            for t in range(PACK):
+                nc.tensor.matmul(
+                    out=agg_bank[:, t, :],
+                    lhsT=h_sb[b][:, K_PASS * g + t : K_PASS * (g + 1) : PACK],
+                    rhs=a_t[:],
+                    start=True,
+                    stop=True,
+                )
+            copy(out=grouped[b][:, GCN, g], in_=agg_bank[:].rearrange("p t n -> p n t"))
 
-        def aggregate(b):
-            agg_grouped[b] = grouped_tile("agg_grouped")
-            for g in range(PASSES):
-                agg_bank = psum.tile([P, PACK, NODES], F32, name="agg_bank", bufs=AGG_BANKS)
-                for t in range(PACK):
-                    nc.tensor.matmul(
-                        out=agg_bank[:, t, :],
-                        lhsT=h_sb[b][:, K_PASS * g + t : K_PASS * (g + 1) : PACK],
-                        rhs=a_t[:],
-                        start=True,
-                        stop=True,
-                    )
-                nc.scalar.copy(out=agg_grouped[b][:, g], in_=agg_bank[:].rearrange("p t n -> p n t"))
-
-        def transpose_attention(b):
-            att_grouped[b] = grouped_tile("att_grouped")
+        def transpose_attention(b, first, last, copy):
             o_pairs = o_sb[b][:].bitcast(F32)
-            for g in range(PASSES):
-                att_bank = psum.tile([P, PAIRS, NODES], F32, name="att_bank", bufs=ATT_BANKS)
+            n = last - first
+            att_bank = psum.tile([P, n, PAIRS, NODES], F32, name="att_bank", bufs=ATT_BANKS)
+            for g in range(first, last):
                 for u in range(PAIRS):
                     nc.tensor.transpose(
-                        att_bank[:, u, :],
+                        att_bank[:, g - first, u, :],
                         o_pairs[:, (K_PASS // 2) * g + u : (K_PASS // 2) * (g + 1) : PAIRS],
                         ident_f32[:],
                     )
-                dst = att_grouped[b][:, g].bitcast(F32)
-                src = att_bank[:].rearrange("p u n -> p n u")
-                if g % 2 == 0 and b < SAMPLES - 1:
-                    nc.vector.tensor_copy(out=dst, in_=src)
-                else:
-                    nc.scalar.copy(out=dst, in_=src)
+            dst = grouped[b][:, ATT, first:last].rearrange("p g n t -> p (g n t)").bitcast(F32)
+            copy(
+                out=dst.rearrange("p (g n u) -> p g n u", g=n, u=PAIRS),
+                in_=att_bank[:].rearrange("p g u n -> p g n u"),
+            )
 
-        def mx_tiles(label):
-            words = per_sample.tile([P, PASSES, NODES], U32, name="%s_words" % label, align_bytes=64)
-            planes = per_sample.tile([P, PASSES, NODES], U8, name="%s_planes" % label, align_bytes=64)
-            return words, planes
-
-        def quantise(grouped, label):
-            words, planes = mx_tiles(label)
+        def quantise(b):
             nc.vector.quantize_mx(
-                out=words[:].rearrange("p g n -> p (g n)").bitcast(FP8X4),
-                scales=planes[:].rearrange("p g n -> p (g n)"),
-                in_=grouped[:].rearrange("p g n t -> p (g n t)"),
+                out=words[b][:].rearrange("p x g n -> p (x g n)").bitcast(FP8X4),
+                scales=planes[b][:].rearrange("p x g n -> p (x g n)"),
+                in_=grouped[b][:].rearrange("p x g n t -> p (x g n t)"),
             )
-            return words, planes
 
-        def quantise_pass(grouped, x_mx, g):
-            words, planes = x_mx
+        def quantise_branch(b, x):
             nc.vector.quantize_mx(
-                out=words[:, g, :].bitcast(FP8X4),
-                scales=planes[:, g, :],
-                in_=grouped[:, g].rearrange("p n t -> p (n t)"),
+                out=words[b][:, x].rearrange("p g n -> p (g n)").bitcast(FP8X4),
+                scales=planes[b][:, x].rearrange("p g n -> p (g n)"),
+                in_=grouped[b][:, x].rearrange("p g n t -> p (g n t)"),
             )
 
-        def multiply_pass(product, x_mx, w_words, w_planes, g):
-            x_words, x_planes = x_mx
-            nc.tensor.matmul_mx(
-                out=product[:],
-                lhsT=x_words[:, g, :].bitcast(FP8X4),
-                lhsT_scale=x_planes[:, g, :],
-                rhs=w_words[:, g, :].bitcast(FP4X4),
-                rhs_scale=w_planes[:, g, :],
-                start=(g == 0),
-                stop=(g == PASSES - 1),
-            )
+        weights = ((gcn_words, gcn_planes), (proj_words, proj_planes))
 
-        def multiply_by_weight(label, banks, x_mx, w_words, w_planes):
-            product = psum.tile([P, OUT_FEATURES], F32, name=label, bufs=banks)
+        def multiply(product, b, x):
+            w_words, w_planes = weights[x]
             for g in range(PASSES):
-                multiply_pass(product, x_mx, w_words, w_planes, g)
-            return product
-
-        def scale_gcn_product(b):
-            scaled[b] = per_sample.tile([P, OUT_FEATURES], F32, name="scaled")
-            nc.vector.tensor_tensor(out=scaled[b][:], in0=gcn_product[b][:], in1=spread[:, 1, :], op=MULT)
-
-        def add_bias(b):
-            gcn_part[b] = per_sample.tile([P, OUT_FEATURES], F32, name="gcn_part")
-            engine = nc.vector if b == LAST else nc.gpsimd
-            engine.tensor_tensor(out=gcn_part[b][:], in0=scaled[b][:], in1=spread[:, 0, :], op=ADD)
-
-        def finish(b):
-            result = per_sample.tile([P, OUT_FEATURES], F32, name="result")
-            nc.vector.tensor_tensor(out=result[:], in0=att_product[b][:], in1=gcn_part[b][:], op=ADD)
-            nc.sync.dma_start(out=out[b], in_=result[:])
-
-        def is_sample(b):
-            return 0 <= b < SAMPLES
-
-        spread = const.tile([P, 2, OUT_FEATURES], F32, name="spread")
-        transpose_attention(0)
-        att_mx[0] = quantise(att_grouped[0], "att")
-        for s in range(SAMPLES + 3):
-            if is_sample(s - 2):
-                scale_gcn_product(s - 2)
-                if 0 < s - 2 < LAST:
-                    att_mx[s - 2] = quantise(att_grouped[s - 2], "att")
-                if s - 2 == LAST:
-                    quantise_pass(att_grouped[LAST], att_mx[LAST], 1)
-                if s - 2 > 0:
-                    add_bias(s - 2)
-            if is_sample(s - 3):
-                finish(s - 3)
-            if is_sample(s):
-                aggregate(s)
-            if is_sample(s - 1) and s - 1 > 0:
-                transpose_attention(s - 1)
-            if s - 2 == 0:
-                add_bias(0)
-            if s - 1 == LAST:
-                att_mx[LAST] = mx_tiles("att")
-                quantise_pass(att_grouped[LAST], att_mx[LAST], 0)
-            if s == 1:
-                spread_bank = psum.tile([P, 2, OUT_FEATURES], F32, name="spread_bank", tag="att_bank", bufs=ATT_BANKS)
-                nc.tensor.matmul(out=spread_bank[:], lhsT=ones[:], rhs=vector_rows[:], start=True, stop=True)
-                nc.scalar.copy(out=spread[:], in_=spread_bank[:])
-            if is_sample(s):
-                agg_mx[s] = quantise(agg_grouped[s], "agg")
-            if is_sample(s - 1):
-                gcn_product[s - 1] = multiply_by_weight(
-                    "gcn_product", GCN_PRODUCT_BANKS, agg_mx[s - 1], gcn_words, gcn_planes
+                nc.tensor.matmul_mx(
+                    out=product,
+                    lhsT=words[b][:, x, g].bitcast(FP8X4),
+                    lhsT_scale=planes[b][:, x, g],
+                    rhs=w_words[:, g, :].bitcast(FP4X4),
+                    rhs_scale=w_planes[:, g, :],
+                    start=(g == 0),
+                    stop=(g == PASSES - 1),
                 )
-            if is_sample(s - 2) and s - 2 < LAST:
-                att_product[s - 2] = multiply_by_weight(
-                    "att_product", ATT_PRODUCT_BANKS, att_mx[s - 2], proj_words, proj_planes
-                )
-            if s - 1 == LAST:
-                att_product[LAST] = psum.tile([P, OUT_FEATURES], F32, name="att_product", bufs=ATT_PRODUCT_BANKS)
-                multiply_pass(att_product[LAST], att_mx[LAST], proj_words, proj_planes, 0)
-            if s - 2 == LAST:
-                multiply_pass(att_product[LAST], att_mx[LAST], proj_words, proj_planes, 1)
+
+        def product_tile(shape, tag="product", bufs=PRODUCT_BANKS):
+            return psum.tile(shape, F32, name="product", tag=tag, bufs=bufs)
+
+        def scale(b, n, gcn_product):
+            scaled = per_sample.tile([P, n, OUT_FEATURES], F32, name="scaled")
+            nc.vector.tensor_tensor(out=scaled[:], in0=gcn_product, in1=spread[:, 1].to_broadcast([P, n, OUT_FEATURES]), op=MULT)
+            return scaled
+
+        def add_bias(b, n, scaled):
+            part = per_sample.tile([P, n, OUT_FEATURES], F32, name="part")
+            nc.gpsimd.tensor_tensor(out=part[:], in0=scaled[:], in1=spread[:, 0].to_broadcast([P, n, OUT_FEATURES]), op=ADD)
+            return part
+
+        def finish(b, n, att_product, part):
+            result = per_sample.tile([P, n, OUT_FEATURES], F32, name="result")
+            nc.vector.tensor_tensor(out=result[:], in0=att_product, in1=part[:], op=ADD)
+            nc.sync.dma_start(out=out[b : b + n].rearrange("b n f -> n b f"), in_=result[:])
+
+        scalar_copy, vector_copy = nc.scalar.copy, nc.vector.tensor_copy
+        transpose_attention(0, 0, 1, scalar_copy)
+        aggregate(0, 0, scalar_copy)
+        transpose_attention(0, 1, 2, vector_copy)
+        aggregate(0, 1, scalar_copy)
+        spread_bank = psum.tile([P, 2, OUT_FEATURES], F32, name="spread_bank", tag="product", bufs=PRODUCT_BANKS)
+        nc.tensor.matmul(out=spread_bank[:], lhsT=ones[:], rhs=vector_rows[:], start=True, stop=True)
+        nc.vector.tensor_copy(out=spread[:, :, 0], in_=spread_bank[:])
+        for b in (1, 2):
+            aggregate(b, 0, vector_copy)
+            aggregate(b, 1, scalar_copy)
+            transpose_attention(b, 0, PASSES, scalar_copy)
+            quantise(b - 1)
+        pair = product_tile([P, 2, 2, OUT_FEATURES])
+        multiply(pair[:, GCN, 0, :], 0, GCN)
+        aggregate(3, 0, scalar_copy)
+        aggregate(3, 1, scalar_copy)
+        multiply(pair[:, GCN, 1, :], 1, GCN)
+        quantise_branch(2, GCN)
+        scaled = scale(0, 2, pair[:, GCN])
+        part = add_bias(0, 2, scaled)
+        transpose_attention(3, 0, PASSES, scalar_copy)
+        quantise_branch(2, ATT)
+        gcn2 = product_tile([P, 1, OUT_FEATURES])
+        multiply(gcn2[:, 0, :], 2, GCN)
+        multiply(pair[:, ATT, 0, :], 0, ATT)
+        multiply(pair[:, ATT, 1, :], 1, ATT)
+        quantise_branch(3, GCN)
+        scaled2 = scale(2, 1, gcn2[:])
+        part2 = add_bias(2, 1, scaled2)
+        finish(0, 2, pair[:, ATT], part)
+        gcn3 = product_tile([P, 1, OUT_FEATURES], "att_bank", ATT_BANKS)
+        multiply(gcn3[:, 0, :], 3, GCN)
+        att2 = product_tile([P, 1, OUT_FEATURES])
+        multiply(att2[:, 0, :], 2, ATT)
+        quantise_branch(3, ATT)
+        scaled3 = scale(3, 1, gcn3[:])
+        part3 = add_bias(3, 1, scaled3)
+        finish(2, 1, att2[:], part2)
+        att3 = product_tile([P, 1, OUT_FEATURES], "agg_bank", AGG_BANKS)
+        multiply(att3[:, 0, :], 3, ATT)
+        finish(3, 1, att3[:], part3)

@@ -102,9 +102,12 @@ def tile_gatblock_pa_s_kernel(
         load(o_sb[3], o_attn[3])
         load_weight(proj_words, proj_planes, w_proj_words, w_proj_scales)
 
-        warm_bank = psum.tile([P, OUT_FEATURES], F32, name="warm_bank", tag="product", bufs=PRODUCT_BANKS)
+        warm_bank = psum.tile([P, 2 * P], F32, name="warm_bank", tag="product", bufs=PRODUCT_BANKS)
+        zeros_bf16 = zeros[:].bitcast(BF16)
+        for i in range(2):
+            nc.tensor.matmul(out=warm_bank[:], lhsT=zeros_bf16[:, 0:P], rhs=zeros_bf16, start=True, stop=True)
         for i in range(WARM_UPS):
-            nc.tensor.matmul(out=warm_bank[:], lhsT=zeros[:], rhs=zeros[:], start=True, stop=True)
+            nc.tensor.matmul(out=warm_bank[:, 0:P], lhsT=zeros[:], rhs=zeros[:], start=True, stop=True)
 
         a_t_bank = psum.tile([P, NODES], BF16, name="a_t_bank", tag="att_bank", bufs=ATT_BANKS)
         nc.tensor.transpose(a_t_bank[:], a_sb[:], ident_bf16[:])

@@ -26,9 +26,9 @@ PAIRS = PACK // 2
 QUADRANTS = 4
 LIVE_ROWS = 4
 
-AGG_BANKS = 4
+AGG_BANKS = 3
 ATT_BANKS = 2
-PRODUCT_BANKS = 2
+PRODUCT_BANKS = 3
 GCN, ATT = 0, 1
 WARM_UPS = 2
 
@@ -198,43 +198,47 @@ def tile_gatblock_pa_s_kernel(
             nc.sync.dma_start(out=out[b : b + n].rearrange("b n f -> n b f"), in_=result[:])
 
         scalar_copy, vector_copy = nc.scalar.copy, nc.vector.tensor_copy
-        transpose_attention(0, 0, 1, scalar_copy)
-        aggregate(0, 0, scalar_copy)
-        transpose_attention(0, 1, 2, vector_copy)
+        transpose_attention(0, 0, 1, vector_copy)
+        aggregate(0, 0, vector_copy)
         aggregate(0, 1, scalar_copy)
+        transpose_attention(0, 1, 2, vector_copy)
+        aggregate(1, 0, vector_copy)
         spread_bank = psum.tile([P, 2, OUT_FEATURES], F32, name="spread_bank", tag="product", bufs=PRODUCT_BANKS)
         nc.tensor.matmul(out=spread_bank[:], lhsT=ones[:], rhs=vector_rows[:], start=True, stop=True)
-        nc.vector.tensor_copy(out=spread[:, :, 0], in_=spread_bank[:])
-        for b in (1, 2):
-            aggregate(b, 0, vector_copy)
-            aggregate(b, 1, scalar_copy)
-            transpose_attention(b, 0, PASSES, scalar_copy)
-            quantise(b - 1)
+        nc.scalar.copy(out=spread[:, :, 0], in_=spread_bank[:])
+        aggregate(1, 1, scalar_copy)
+        transpose_attention(1, 0, PASSES, scalar_copy)
+        quantise(0)
+        quantise_branch(1, GCN)
+        aggregate(2, 0, scalar_copy)
+        transpose_attention(2, 0, PASSES, scalar_copy)
         pair = product_tile([P, 2, 2, OUT_FEATURES])
         multiply(pair[:, GCN, 0, :], 0, GCN)
-        aggregate(3, 0, scalar_copy)
-        aggregate(3, 1, scalar_copy)
         multiply(pair[:, GCN, 1, :], 1, GCN)
-        quantise_branch(2, GCN)
+        quantise_branch(1, ATT)
         scaled = scale(0, 2, pair[:, GCN])
         part = add_bias(0, 2, scaled)
+        aggregate(2, 1, vector_copy)
+        aggregate(3, 0, scalar_copy)
+        aggregate(3, 1, scalar_copy)
         transpose_attention(3, 0, PASSES, scalar_copy)
-        quantise_branch(2, ATT)
-        gcn2 = product_tile([P, 1, OUT_FEATURES])
-        multiply(gcn2[:, 0, :], 2, GCN)
         multiply(pair[:, ATT, 0, :], 0, ATT)
         multiply(pair[:, ATT, 1, :], 1, ATT)
+        quantise_branch(2, GCN)
+        quantise_branch(2, ATT)
         quantise_branch(3, GCN)
-        scaled2 = scale(2, 1, gcn2[:])
-        part2 = add_bias(2, 1, scaled2)
-        finish(0, 2, pair[:, ATT], part)
+        gcn2 = product_tile([P, 1, OUT_FEATURES])
+        multiply(gcn2[:, 0, :], 2, GCN)
         gcn3 = product_tile([P, 1, OUT_FEATURES], "att_bank", ATT_BANKS)
         multiply(gcn3[:, 0, :], 3, GCN)
-        att2 = product_tile([P, 1, OUT_FEATURES])
-        multiply(att2[:, 0, :], 2, ATT)
+        scaled2 = scale(2, 1, gcn2[:])
+        part2 = add_bias(2, 1, scaled2)
         quantise_branch(3, ATT)
         scaled3 = scale(3, 1, gcn3[:])
         part3 = add_bias(3, 1, scaled3)
+        att2 = product_tile([P, 1, OUT_FEATURES])
+        multiply(att2[:, 0, :], 2, ATT)
+        finish(0, 2, pair[:, ATT], part)
         finish(2, 1, att2[:], part2)
         att3 = product_tile([P, 1, OUT_FEATURES], "agg_bank", AGG_BANKS)
         multiply(att3[:, 0, :], 3, ATT)

@@ -26,9 +26,9 @@ PAIRS = PACK // 2
 QUADRANTS = 4
 LIVE_ROWS = 4
 
-AGG_BANKS = 3
+AGG_BANKS = 4
 ATT_BANKS = 2
-PRODUCT_BANKS = 3
+PRODUCT_BANKS = 2
 GCN, ATT = 0, 1
 WARM_UPS = 2
 
@@ -88,38 +88,34 @@ def tile_gatblock_pa_s_kernel(
             nc.sync.dma_start(out=tile[:, first:last], in_=dram[:, first:last])
 
         nc.sync.dma_start(out=a_sb[:], in_=a_gcn)
-        load(o_sb[0], o_attn[0], 0, K_PASS)
         load(h_sb[0], h_norm[0])
-        load(o_sb[0], o_attn[0], K_PASS, FEATURES)
         load(h_sb[1], h_norm[1])
         nc.sync.dma_start(out=vector_rows[0:1, 0, :], in_=b_proj.unsqueeze(0))
         nc.sync.dma_start(out=vector_rows[0:1, 1, :], in_=gcn_m.unsqueeze(0))
-        load(o_sb[1], o_attn[1])
         load(h_sb[2], h_norm[2])
-        load(o_sb[2], o_attn[2])
-        load_weight(gcn_words, gcn_planes, gcn_w_words, gcn_w_scales)
         load(h_sb[3], h_norm[3])
-        load(o_sb[3], o_attn[3])
+        load_weight(gcn_words, gcn_planes, gcn_w_words, gcn_w_scales)
+        for b in range(SAMPLES):
+            load(o_sb[b], o_attn[b])
         load_weight(proj_words, proj_planes, w_proj_words, w_proj_scales)
 
-        warm_bank = psum.tile([P, 2 * P], F32, name="warm_bank", tag="product", bufs=PRODUCT_BANKS)
-        zeros_bf16 = zeros[:].bitcast(BF16)
-        for i in range(2):
-            nc.tensor.matmul(out=warm_bank[:], lhsT=zeros_bf16[:, 0:P], rhs=zeros_bf16, start=True, stop=True)
+        warm_bank = psum.tile([P, P], F32, name="warm_bank", tag="product", bufs=PRODUCT_BANKS)
         for i in range(WARM_UPS):
-            nc.tensor.matmul(out=warm_bank[:, 0:P], lhsT=zeros[:], rhs=zeros[:], start=True, stop=True)
+            nc.tensor.matmul(out=warm_bank[:], lhsT=zeros[:], rhs=zeros[:], start=True, stop=True)
 
         a_t_bank = psum.tile([P, NODES], BF16, name="a_t_bank", tag="att_bank", bufs=ATT_BANKS)
         nc.tensor.transpose(a_t_bank[:], a_sb[:], ident_bf16[:])
+        nc.tensor.matmul(out=warm_bank[:], lhsT=zeros[:], rhs=zeros[:], start=True, stop=True)
         a_t = const.tile([P, NODES], BF16, name="a_t")
         nc.vector.tensor_copy(out=a_t[:], in_=a_t_bank[:])
         spread = const.tile([P, 2, 1, OUT_FEATURES], F32, name="spread")
 
-        grouped, words, planes = [], [], []
-        for b in range(SAMPLES):
-            grouped.append(per_sample.tile([P, 2, PASSES, NODES, PACK], BF16, name="grouped", align_bytes=64))
-            words.append(per_sample.tile([P, 2, PASSES, NODES], U32, name="words", align_bytes=64))
-            planes.append(per_sample.tile([P, 2, PASSES, NODES], U8, name="planes", align_bytes=64))
+        grouped, words, planes = {}, {}, {}
+        for x in (GCN, ATT):
+            for q in range(2):
+                grouped[x, q] = per_sample.tile([P, 2, PASSES, NODES, PACK], BF16, name="grouped", align_bytes=64)
+                words[x, q] = per_sample.tile([P, 2, PASSES, NODES], U32, name="words", align_bytes=64)
+                planes[x, q] = per_sample.tile([P, 2, PASSES, NODES], U8, name="planes", align_bytes=64)
 
         def aggregate(b, g, copy):
             agg_bank = psum.tile([P, PACK, NODES], F32, name="agg_bank", bufs=AGG_BANKS)
@@ -131,7 +127,7 @@ def tile_gatblock_pa_s_kernel(
                     start=True,
                     stop=True,
                 )
-            copy(out=grouped[b][:, GCN, g], in_=agg_bank[:].rearrange("p t n -> p n t"))
+            copy(out=grouped[GCN, b // 2][:, b % 2, g], in_=agg_bank[:].rearrange("p t n -> p n t"))
 
         def transpose_attention(b, first, last, copy):
             o_pairs = o_sb[b][:].bitcast(F32)
@@ -144,24 +140,25 @@ def tile_gatblock_pa_s_kernel(
                         o_pairs[:, (K_PASS // 2) * g + u : (K_PASS // 2) * (g + 1) : PAIRS],
                         ident_f32[:],
                     )
-            dst = grouped[b][:, ATT, first:last].rearrange("p g n t -> p (g n t)").bitcast(F32)
+            dst = grouped[ATT, b // 2][:, b % 2, first:last].rearrange("p g n t -> p (g n t)").bitcast(F32)
             copy(
                 out=dst.rearrange("p (g n u) -> p g n u", g=n, u=PAIRS),
                 in_=att_bank[:].rearrange("p g u n -> p g n u"),
             )
 
-        def quantise(b):
+        def quantise_pair(x, q):
             nc.vector.quantize_mx(
-                out=words[b][:].rearrange("p x g n -> p (x g n)").bitcast(FP8X4),
-                scales=planes[b][:].rearrange("p x g n -> p (x g n)"),
-                in_=grouped[b][:].rearrange("p x g n t -> p (x g n t)"),
+                out=words[x, q][:].rearrange("p s g n -> p (s g n)").bitcast(FP8X4),
+                scales=planes[x, q][:].rearrange("p s g n -> p (s g n)"),
+                in_=grouped[x, q][:].rearrange("p s g n t -> p (s g n t)"),
             )
 
-        def quantise_branch(b, x):
+        def quantise(x, b):
+            q, s = b // 2, b % 2
             nc.vector.quantize_mx(
-                out=words[b][:, x].rearrange("p g n -> p (g n)").bitcast(FP8X4),
-                scales=planes[b][:, x].rearrange("p g n -> p (g n)"),
-                in_=grouped[b][:, x].rearrange("p g n t -> p (g n t)"),
+                out=words[x, q][:, s].rearrange("p g n -> p (g n)").bitcast(FP8X4),
+                scales=planes[x, q][:, s].rearrange("p g n -> p (g n)"),
+                in_=grouped[x, q][:, s].rearrange("p g n t -> p (g n t)"),
             )
 
         weights = ((gcn_words, gcn_planes), (proj_words, proj_planes))
@@ -171,8 +168,8 @@ def tile_gatblock_pa_s_kernel(
             for g in range(PASSES):
                 nc.tensor.matmul_mx(
                     out=product,
-                    lhsT=words[b][:, x, g].bitcast(FP8X4),
-                    lhsT_scale=planes[b][:, x, g],
+                    lhsT=words[x, b // 2][:, b % 2, g].bitcast(FP8X4),
+                    lhsT_scale=planes[x, b // 2][:, b % 2, g],
                     rhs=w_words[:, g, :].bitcast(FP4X4),
                     rhs_scale=w_planes[:, g, :],
                     start=(g == 0),
@@ -194,52 +191,48 @@ def tile_gatblock_pa_s_kernel(
 
         def finish(b, n, att_product, part):
             result = per_sample.tile([P, n, OUT_FEATURES], F32, name="result")
-            nc.vector.tensor_tensor(out=result[:], in0=att_product, in1=part[:], op=ADD)
+            nc.vector.tensor_tensor(out=result[:], in0=att_product, in1=part, op=ADD)
             nc.sync.dma_start(out=out[b : b + n].rearrange("b n f -> n b f"), in_=result[:])
 
         scalar_copy, vector_copy = nc.scalar.copy, nc.vector.tensor_copy
-        transpose_attention(0, 0, 1, vector_copy)
         aggregate(0, 0, vector_copy)
         aggregate(0, 1, scalar_copy)
-        transpose_attention(0, 1, 2, vector_copy)
         aggregate(1, 0, vector_copy)
+        aggregate(1, 1, scalar_copy)
+        aggregate(2, 0, scalar_copy)
+        aggregate(2, 1, scalar_copy)
+        quantise_pair(GCN, 0)
+        aggregate(3, 0, vector_copy)
+        aggregate(3, 1, scalar_copy)
         spread_bank = psum.tile([P, 2, OUT_FEATURES], F32, name="spread_bank", tag="product", bufs=PRODUCT_BANKS)
         nc.tensor.matmul(out=spread_bank[:], lhsT=ones[:], rhs=vector_rows[:], start=True, stop=True)
         nc.scalar.copy(out=spread[:, :, 0], in_=spread_bank[:])
-        aggregate(1, 1, scalar_copy)
+        transpose_attention(0, 0, PASSES, scalar_copy)
+        gcn01 = product_tile([P, 2, OUT_FEATURES])
+        multiply(gcn01[:, 0, :], 0, GCN)
+        multiply(gcn01[:, 1, :], 1, GCN)
+        quantise_pair(GCN, 1)
         transpose_attention(1, 0, PASSES, scalar_copy)
-        quantise(0)
-        quantise_branch(1, GCN)
-        aggregate(2, 0, scalar_copy)
+        scaled01 = scale(0, 2, gcn01[:])
+        part01 = add_bias(0, 2, scaled01)
+        quantise(ATT, 0)
+        gcn23 = product_tile([P, 2, OUT_FEATURES])
+        multiply(gcn23[:, 0, :], 2, GCN)
+        multiply(gcn23[:, 1, :], 3, GCN)
+        scaled23 = scale(2, 2, gcn23[:])
+        part23 = add_bias(2, 2, scaled23)
+        quantise(ATT, 1)
         transpose_attention(2, 0, PASSES, scalar_copy)
-        pair = product_tile([P, 2, 2, OUT_FEATURES])
-        multiply(pair[:, GCN, 0, :], 0, GCN)
-        multiply(pair[:, GCN, 1, :], 1, GCN)
-        quantise_branch(1, ATT)
-        scaled = scale(0, 2, pair[:, GCN])
-        part = add_bias(0, 2, scaled)
-        aggregate(2, 1, vector_copy)
-        aggregate(3, 0, scalar_copy)
-        aggregate(3, 1, scalar_copy)
         transpose_attention(3, 0, PASSES, scalar_copy)
-        multiply(pair[:, ATT, 0, :], 0, ATT)
-        multiply(pair[:, ATT, 1, :], 1, ATT)
-        quantise_branch(2, GCN)
-        quantise_branch(2, ATT)
-        quantise_branch(3, GCN)
-        gcn2 = product_tile([P, 1, OUT_FEATURES])
-        multiply(gcn2[:, 0, :], 2, GCN)
-        gcn3 = product_tile([P, 1, OUT_FEATURES], "att_bank", ATT_BANKS)
-        multiply(gcn3[:, 0, :], 3, GCN)
-        scaled2 = scale(2, 1, gcn2[:])
-        part2 = add_bias(2, 1, scaled2)
-        quantise_branch(3, ATT)
-        scaled3 = scale(3, 1, gcn3[:])
-        part3 = add_bias(3, 1, scaled3)
+        att01 = product_tile([P, 2, OUT_FEATURES])
+        multiply(att01[:, 0, :], 0, ATT)
+        multiply(att01[:, 1, :], 1, ATT)
+        quantise(ATT, 2)
         att2 = product_tile([P, 1, OUT_FEATURES])
         multiply(att2[:, 0, :], 2, ATT)
-        finish(0, 2, pair[:, ATT], part)
-        finish(2, 1, att2[:], part2)
+        quantise(ATT, 3)
+        finish(0, 2, att01[:], part01[:])
         att3 = product_tile([P, 1, OUT_FEATURES], "agg_bank", AGG_BANKS)
         multiply(att3[:, 0, :], 3, ATT)
-        finish(3, 1, att3[:], part3)
+        finish(2, 1, att2[:], part23[:, 0:1])
+        finish(3, 1, att3[:], part23[:, 1:2])

@@ -94,18 +94,22 @@ def tile_gatblock_pa_s_kernel(
         nc.sync.dma_start(out=vector_rows[0:1, 1, :], in_=gcn_m.unsqueeze(0))
         load(h_sb[2], h_norm[2])
         load(h_sb[3], h_norm[3])
+        load(o_sb[0], o_attn[0])
         load_weight(gcn_words, gcn_planes, gcn_w_words, gcn_w_scales)
-        for b in range(SAMPLES):
+        for b in range(1, SAMPLES):
             load(o_sb[b], o_attn[b])
         load_weight(proj_words, proj_planes, w_proj_words, w_proj_scales)
 
-        warm_bank = psum.tile([P, P], F32, name="warm_bank", tag="product", bufs=PRODUCT_BANKS)
-        for i in range(WARM_UPS):
-            nc.tensor.matmul(out=warm_bank[:], lhsT=zeros[:], rhs=zeros[:], start=True, stop=True)
+        def keep_clock(n, tag, bufs):
+            bank = psum.tile([P, P], F32, name="warm_bank", tag=tag, bufs=bufs)
+            for i in range(n):
+                nc.tensor.matmul(out=bank[:], lhsT=zeros[:], rhs=zeros[:], start=True, stop=True)
+
+        keep_clock(WARM_UPS, "product", PRODUCT_BANKS)
 
         a_t_bank = psum.tile([P, NODES], BF16, name="a_t_bank", tag="att_bank", bufs=ATT_BANKS)
         nc.tensor.transpose(a_t_bank[:], a_sb[:], ident_bf16[:])
-        nc.tensor.matmul(out=warm_bank[:], lhsT=zeros[:], rhs=zeros[:], start=True, stop=True)
+        keep_clock(1, "agg_bank", AGG_BANKS)
         a_t = const.tile([P, NODES], BF16, name="a_t")
         nc.vector.tensor_copy(out=a_t[:], in_=a_t_bank[:])
         spread = const.tile([P, 2, 1, OUT_FEATURES], F32, name="spread")
@@ -184,9 +188,9 @@ def tile_gatblock_pa_s_kernel(
             nc.vector.tensor_tensor(out=scaled[:], in0=gcn_product, in1=spread[:, 1].to_broadcast([P, n, OUT_FEATURES]), op=MULT)
             return scaled
 
-        def add_bias(b, n, scaled):
+        def add_bias(b, n, scaled, engine):
             part = per_sample.tile([P, n, OUT_FEATURES], F32, name="part")
-            nc.gpsimd.tensor_tensor(out=part[:], in0=scaled[:], in1=spread[:, 0].to_broadcast([P, n, OUT_FEATURES]), op=ADD)
+            engine.tensor_tensor(out=part[:], in0=scaled[:], in1=spread[:, 0].to_broadcast([P, n, OUT_FEATURES]), op=ADD)
             return part
 
         def finish(b, n, att_product, part):
@@ -202,32 +206,34 @@ def tile_gatblock_pa_s_kernel(
         aggregate(2, 0, scalar_copy)
         aggregate(2, 1, scalar_copy)
         quantise_pair(GCN, 0)
-        aggregate(3, 0, vector_copy)
-        aggregate(3, 1, scalar_copy)
         spread_bank = psum.tile([P, 2, OUT_FEATURES], F32, name="spread_bank", tag="product", bufs=PRODUCT_BANKS)
         nc.tensor.matmul(out=spread_bank[:], lhsT=ones[:], rhs=vector_rows[:], start=True, stop=True)
-        nc.scalar.copy(out=spread[:, :, 0], in_=spread_bank[:])
+        nc.vector.tensor_copy(out=spread[:, :, 0], in_=spread_bank[:])
+        aggregate(3, 0, vector_copy)
+        aggregate(3, 1, scalar_copy)
         transpose_attention(0, 0, PASSES, scalar_copy)
         gcn01 = product_tile([P, 2, OUT_FEATURES])
         multiply(gcn01[:, 0, :], 0, GCN)
         multiply(gcn01[:, 1, :], 1, GCN)
+        scaled01 = scale(0, 2, gcn01[:])
+        keep_clock(1, "agg_bank", AGG_BANKS)
         quantise_pair(GCN, 1)
         transpose_attention(1, 0, PASSES, scalar_copy)
-        scaled01 = scale(0, 2, gcn01[:])
-        part01 = add_bias(0, 2, scaled01)
+        part01 = add_bias(0, 2, scaled01, nc.vector)
         quantise(ATT, 0)
+        transpose_attention(2, 0, PASSES, scalar_copy)
         gcn23 = product_tile([P, 2, OUT_FEATURES])
         multiply(gcn23[:, 0, :], 2, GCN)
         multiply(gcn23[:, 1, :], 3, GCN)
-        scaled23 = scale(2, 2, gcn23[:])
-        part23 = add_bias(2, 2, scaled23)
         quantise(ATT, 1)
-        transpose_attention(2, 0, PASSES, scalar_copy)
+        scaled23 = scale(2, 2, gcn23[:])
+        part23 = add_bias(2, 2, scaled23, nc.gpsimd)
+        quantise(ATT, 2)
         transpose_attention(3, 0, PASSES, scalar_copy)
         att01 = product_tile([P, 2, OUT_FEATURES])
         multiply(att01[:, 0, :], 0, ATT)
         multiply(att01[:, 1, :], 1, ATT)
-        quantise(ATT, 2)
+        keep_clock(1, "agg_bank", AGG_BANKS)
         att2 = product_tile([P, 1, OUT_FEATURES])
         multiply(att2[:, 0, :], 2, ATT)
         quantise(ATT, 3)

@@ -26,9 +26,7 @@ PAIRS = PACK // 2
 QUADRANTS = 4
 LIVE_ROWS = 4
 
-AGG_BANKS = 4
-ATT_BANKS = 2
-PRODUCT_BANKS = 2
+BANKS = {"agg": 4, "att": 2, "product": 2}
 GCN, ATT = 0, 1
 WARM_UPS = 2
 
@@ -44,6 +42,13 @@ def tile_gatblock_pa_s_kernel(
         const = ctx.enter_context(tc.tile_pool(name="const", bufs=1))
         per_sample = ctx.enter_context(tc.tile_pool(name="per_sample", bufs=SAMPLES))
         psum = ctx.enter_context(tc.psum_pool(name="psum", bufs=1))
+        turns = {"agg": 0, "att": 0, "product": 0}
+
+        def bank_tile(shape, dtype, kind):
+            turn = turns[kind] % BANKS[kind]
+            turns[kind] += 1
+            return psum.tile(shape, dtype, name="%s_bank" % kind, tag="%s_%d" % (kind, turn))
+
 
         zeros = const.tile([P, P], F32, name="zeros")
         nc.vector.memset(zeros[:], 0.0)
@@ -100,16 +105,16 @@ def tile_gatblock_pa_s_kernel(
             load(o_sb[b], o_attn[b])
         load_weight(proj_words, proj_planes, w_proj_words, w_proj_scales)
 
-        def keep_clock(n, tag, bufs):
-            bank = psum.tile([P, P], F32, name="warm_bank", tag=tag, bufs=bufs)
+        def keep_clock(n, tag):
+            bank = bank_tile([P, P], F32, tag)
             for i in range(n):
                 nc.tensor.matmul(out=bank[:], lhsT=zeros[:], rhs=zeros[:], start=True, stop=True)
 
-        keep_clock(WARM_UPS, "product", PRODUCT_BANKS)
+        keep_clock(WARM_UPS, "product")
 
-        a_t_bank = psum.tile([P, NODES], BF16, name="a_t_bank", tag="att_bank", bufs=ATT_BANKS)
+        a_t_bank = bank_tile([P, NODES], BF16, "att")
         nc.tensor.transpose(a_t_bank[:], a_sb[:], ident_bf16[:])
-        keep_clock(1, "agg_bank", AGG_BANKS)
+        keep_clock(1, "product")
         a_t = const.tile([P, NODES], BF16, name="a_t")
         nc.vector.tensor_copy(out=a_t[:], in_=a_t_bank[:])
         spread = const.tile([P, 2, 1, OUT_FEATURES], F32, name="spread")
@@ -122,7 +127,7 @@ def tile_gatblock_pa_s_kernel(
                 planes[x, q] = per_sample.tile([P, 2, PASSES, NODES], U8, name="planes", align_bytes=64)
 
         def aggregate(b, g, copy):
-            agg_bank = psum.tile([P, PACK, NODES], F32, name="agg_bank", bufs=AGG_BANKS)
+            agg_bank = bank_tile([P, PACK, NODES], F32, "agg")
             for t in range(PACK):
                 nc.tensor.matmul(
                     out=agg_bank[:, t, :],
@@ -136,7 +141,7 @@ def tile_gatblock_pa_s_kernel(
         def transpose_attention(b, first, last, copy):
             o_pairs = o_sb[b][:].bitcast(F32)
             n = last - first
-            att_bank = psum.tile([P, n, PAIRS, NODES], F32, name="att_bank", bufs=ATT_BANKS)
+            att_bank = bank_tile([P, n, PAIRS, NODES], F32, "att")
             for g in range(first, last):
                 for u in range(PAIRS):
                     nc.tensor.transpose(
@@ -180,8 +185,21 @@ def tile_gatblock_pa_s_kernel(
                     stop=(g == PASSES - 1),
                 )
 
-        def product_tile(shape, tag="product", bufs=PRODUCT_BANKS):
-            return psum.tile(shape, F32, name="product", tag=tag, bufs=bufs)
+        def repeat_pass(n):
+            bank = bank_tile([P, OUT_FEATURES], F32, "agg")
+            for i in range(n):
+                nc.tensor.matmul_mx(
+                    out=bank[:],
+                    lhsT=words[GCN, 0][:, 0, 0].bitcast(FP8X4),
+                    lhsT_scale=planes[GCN, 0][:, 0, 0],
+                    rhs=gcn_words[:, 0, :].bitcast(FP4X4),
+                    rhs_scale=gcn_planes[:, 0, :],
+                    start=True,
+                    stop=True,
+                )
+
+        def product_tile(shape, tag="product"):
+            return bank_tile(shape, F32, tag)
 
         def scale(b, n, gcn_product):
             scaled = per_sample.tile([P, n, OUT_FEATURES], F32, name="scaled")
@@ -206,7 +224,7 @@ def tile_gatblock_pa_s_kernel(
         aggregate(2, 0, scalar_copy)
         aggregate(2, 1, scalar_copy)
         quantise_pair(GCN, 0)
-        spread_bank = psum.tile([P, 2, OUT_FEATURES], F32, name="spread_bank", tag="product", bufs=PRODUCT_BANKS)
+        spread_bank = bank_tile([P, 2, OUT_FEATURES], F32, "product")
         nc.tensor.matmul(out=spread_bank[:], lhsT=ones[:], rhs=vector_rows[:], start=True, stop=True)
         nc.vector.tensor_copy(out=spread[:, :, 0], in_=spread_bank[:])
         aggregate(3, 0, vector_copy)
@@ -216,7 +234,7 @@ def tile_gatblock_pa_s_kernel(
         multiply(gcn01[:, 0, :], 0, GCN)
         multiply(gcn01[:, 1, :], 1, GCN)
         scaled01 = scale(0, 2, gcn01[:])
-        keep_clock(1, "agg_bank", AGG_BANKS)
+        repeat_pass(4)
         quantise_pair(GCN, 1)
         transpose_attention(1, 0, PASSES, scalar_copy)
         part01 = add_bias(0, 2, scaled01, nc.vector)
@@ -233,12 +251,12 @@ def tile_gatblock_pa_s_kernel(
         att01 = product_tile([P, 2, OUT_FEATURES])
         multiply(att01[:, 0, :], 0, ATT)
         multiply(att01[:, 1, :], 1, ATT)
-        keep_clock(1, "agg_bank", AGG_BANKS)
+        repeat_pass(4)
         att2 = product_tile([P, 1, OUT_FEATURES])
         multiply(att2[:, 0, :], 2, ATT)
         quantise(ATT, 3)
         finish(0, 2, att01[:], part01[:])
-        att3 = product_tile([P, 1, OUT_FEATURES], "agg_bank", AGG_BANKS)
+        att3 = product_tile([P, 1, OUT_FEATURES], "agg")
         multiply(att3[:, 0, :], 3, ATT)
         finish(2, 1, att2[:], part23[:, 0:1])
         finish(3, 1, att3[:], part23[:, 1:2])

@@ -141,7 +141,7 @@ def tile_gatblock_pa_s_kernel(
         def transpose_attention(b, first, last, copy):
             o_pairs = o_sb[b][:].bitcast(F32)
             n = last - first
-            att_bank = bank_tile([P, n, PAIRS, NODES], F32, "att")
+            att_bank = bank_tile([P, n, PAIRS, NODES], F32, "att" if b < 2 else "agg")
             for g in range(first, last):
                 for u in range(PAIRS):
                     nc.tensor.transpose(
@@ -234,7 +234,7 @@ def tile_gatblock_pa_s_kernel(
         multiply(gcn01[:, 0, :], 0, GCN)
         multiply(gcn01[:, 1, :], 1, GCN)
         scaled01 = scale(0, 2, gcn01[:])
-        repeat_pass(4)
+        repeat_pass(5)
         quantise_pair(GCN, 1)
         transpose_attention(1, 0, PASSES, scalar_copy)
         part01 = add_bias(0, 2, scaled01, nc.vector)

@@ -245,7 +245,6 @@ def tile_gatblock_pa_s_kernel(
         multiply(gcn23[:, 1, :], 3, GCN)
         quantise(ATT, 1)
         scaled23 = scale(2, 2, gcn23[:])
-        part23 = add_bias(2, 2, scaled23, nc.gpsimd)
         quantise(ATT, 2)
         transpose_attention(3, 0, PASSES, scalar_copy)
         att01 = product_tile([P, 2, OUT_FEATURES])
@@ -254,6 +253,7 @@ def tile_gatblock_pa_s_kernel(
         repeat_pass(4)
         att2 = product_tile([P, 1, OUT_FEATURES])
         multiply(att2[:, 0, :], 2, ATT)
+        part23 = add_bias(2, 2, scaled23, nc.vector)
         quantise(ATT, 3)
         finish(0, 2, att01[:], part01[:])
         att3 = product_tile([P, 1, OUT_FEATURES], "agg")

from contextlib import ExitStack

import concourse.mybir as mybir
from concourse.masks import make_identity

BF16 = mybir.dt.bfloat16
F32 = mybir.dt.float32
I32 = mybir.dt.int32
U32 = mybir.dt.uint32
U8 = mybir.dt.uint8
FP8X4 = mybir.dt.float8_e4m3fn_x4
FP4X4 = mybir.dt.float4_e2m1fn_x4
MULT = mybir.AluOpType.mult
ADD = mybir.AluOpType.add

P = 128
SAMPLES = 4
LAST = SAMPLES - 1
NODES = 128
FEATURES = 1024
OUT_FEATURES = 128
PACK = 4
K_PASS = P * PACK
PASSES = FEATURES // K_PASS
PAIRS = PACK // 2
QUADRANTS = 4
LIVE_ROWS = 4

BANKS = {"agg": 4, "att": 2, "product": 2}
GCN, ATT = 0, 1
WARM_UPS = 2

FLOPS = 2 * (2 * SAMPLES * NODES * FEATURES * OUT_FEATURES) + 2 * SAMPLES * NODES * NODES * FEATURES


def tile_gatblock_pa_s_kernel(
    tc, h_norm, o_attn, a_gcn, w_proj_words, w_proj_scales, b_proj, gcn_w_words, gcn_w_scales, gcn_m, out
):
    nc = tc.nc
    with ExitStack() as ctx:
        ctx.enter_context(tc.manual_schedule())
        const = ctx.enter_context(tc.tile_pool(name="const", bufs=1))
        per_sample = ctx.enter_context(tc.tile_pool(name="per_sample", bufs=SAMPLES))
        psum = ctx.enter_context(tc.psum_pool(name="psum", bufs=1))
        turns = {"agg": 0, "att": 0, "product": 0}

        def bank_tile(shape, dtype, kind):
            turn = turns[kind] % BANKS[kind]
            turns[kind] += 1
            return psum.tile(shape, dtype, name="%s_bank" % kind, tag="%s_%d" % (kind, turn))


        zeros = const.tile([P, P], F32, name="zeros")
        nc.vector.memset(zeros[:], 0.0)
        ident_f32 = const.tile([P, P], F32, name="ident_f32")
        make_identity(nc, ident_f32[:])
        ones = const.tile([P, P], BF16, name="ones")
        nc.vector.memset(ones[:], 1.0)
        vector_rows = const.tile([P, 2, OUT_FEATURES], BF16, name="vector_rows")
        nc.vector.memset(vector_rows[:], 0.0)

        def weight_tiles(label):
            words = const.tile([P, PASSES, 2 * OUT_FEATURES], U8, name="%s_words" % label, align_bytes=64)
            planes = const.tile([P, PASSES, OUT_FEATURES], U8, name="%s_planes" % label, align_bytes=64)
            nc.vector.memset(planes[:].bitcast(I32), 0)
            return words, planes

        def load_weight(words, planes, dram_words, dram_scales):
            nc.sync.dma_start(out=words[:].bitcast(I32), in_=dram_words.rearrange("g p c -> p g c").bitcast(I32))
            for quadrant in range(QUADRANTS):
                nc.sync.dma_start(
                    out=planes[32 * quadrant : 32 * quadrant + LIVE_ROWS].bitcast(I32),
                    in_=dram_scales[:, LIVE_ROWS * quadrant : LIVE_ROWS * (quadrant + 1), :]
                    .rearrange("g r n -> r g n")
                    .bitcast(I32),
                )

        def load_sample(dram, b, label):
            x_sb = per_sample.tile([P, FEATURES], BF16, name=label)
            nc.sync.dma_start(out=x_sb[:], in_=dram[b])
            return x_sb

        gcn_words, gcn_planes = weight_tiles("gcn")
        proj_words, proj_planes = weight_tiles("proj")
        ident_bf16 = const.tile([P, P], BF16, name="ident_bf16")
        nc.vector.tensor_copy(out=ident_bf16[:], in_=ident_f32[:])

        a_sb = const.tile([P, NODES], BF16, name="a_sb")
        h_sb = [per_sample.tile([P, FEATURES], BF16, name="h_sb") for b in range(SAMPLES)]
        o_sb = [per_sample.tile([P, FEATURES], BF16, name="o_sb") for b in range(SAMPLES)]

        def load(tile, dram, first=0, last=FEATURES):
            nc.sync.dma_start(out=tile[:, first:last], in_=dram[:, first:last])

        nc.sync.dma_start(out=a_sb[:], in_=a_gcn)
        load(h_sb[0], h_norm[0])
        load(h_sb[1], h_norm[1])
        nc.sync.dma_start(out=vector_rows[0:1, 0, :], in_=b_proj.unsqueeze(0))
        nc.sync.dma_start(out=vector_rows[0:1, 1, :], in_=gcn_m.unsqueeze(0))
        load(h_sb[2], h_norm[2])
        load(h_sb[3], h_norm[3])
        load(o_sb[0], o_attn[0])
        load_weight(gcn_words, gcn_planes, gcn_w_words, gcn_w_scales)
        for b in range(1, SAMPLES):
            load(o_sb[b], o_attn[b])
        load_weight(proj_words, proj_planes, w_proj_words, w_proj_scales)

        def keep_clock(n, tag):
            bank = bank_tile([P, P], F32, tag)
            for i in range(n):
                nc.tensor.matmul(out=bank[:], lhsT=zeros[:], rhs=zeros[:], start=True, stop=True)

        keep_clock(WARM_UPS, "product")

        a_t_bank = bank_tile([P, NODES], BF16, "att")
        nc.tensor.transpose(a_t_bank[:], a_sb[:], ident_bf16[:])
        keep_clock(1, "product")
        a_t = const.tile([P, NODES], BF16, name="a_t")
        nc.vector.tensor_copy(out=a_t[:], in_=a_t_bank[:])
        spread = const.tile([P, 2, 1, OUT_FEATURES], F32, name="spread")

        grouped, words, planes = {}, {}, {}
        for x in (GCN, ATT):
            for q in range(2):
                grouped[x, q] = per_sample.tile([P, 2, PASSES, NODES, PACK], BF16, name="grouped", align_bytes=64)
                words[x, q] = per_sample.tile([P, 2, PASSES, NODES], U32, name="words", align_bytes=64)
                planes[x, q] = per_sample.tile([P, 2, PASSES, NODES], U8, name="planes", align_bytes=64)

        def aggregate(b, g, copy):
            agg_bank = bank_tile([P, PACK, NODES], F32, "agg")
            for t in range(PACK):
                nc.tensor.matmul(
                    out=agg_bank[:, t, :],
                    lhsT=h_sb[b][:, K_PASS * g + t : K_PASS * (g + 1) : PACK],
                    rhs=a_t[:],
                    start=True,
                    stop=True,
                )
            copy(out=grouped[GCN, b // 2][:, b % 2, g], in_=agg_bank[:].rearrange("p t n -> p n t"))

        def transpose_attention(b, first, last, copy):
            o_pairs = o_sb[b][:].bitcast(F32)
            n = last - first
            att_bank = bank_tile([P, n, PAIRS, NODES], F32, "att" if b < 2 else "agg")
            for g in range(first, last):
                for u in range(PAIRS):
                    nc.tensor.transpose(
                        att_bank[:, g - first, u, :],
                        o_pairs[:, (K_PASS // 2) * g + u : (K_PASS // 2) * (g + 1) : PAIRS],
                        ident_f32[:],
                    )
            dst = grouped[ATT, b // 2][:, b % 2, first:last].rearrange("p g n t -> p (g n t)").bitcast(F32)
            copy(
                out=dst.rearrange("p (g n u) -> p g n u", g=n, u=PAIRS),
                in_=att_bank[:].rearrange("p g u n -> p g n u"),
            )

        def quantise_pair(x, q):
            nc.vector.quantize_mx(
                out=words[x, q][:].rearrange("p s g n -> p (s g n)").bitcast(FP8X4),
                scales=planes[x, q][:].rearrange("p s g n -> p (s g n)"),
                in_=grouped[x, q][:].rearrange("p s g n t -> p (s g n t)"),
            )

        def quantise(x, b):
            q, s = b // 2, b % 2
            nc.vector.quantize_mx(
                out=words[x, q][:, s].rearrange("p g n -> p (g n)").bitcast(FP8X4),
                scales=planes[x, q][:, s].rearrange("p g n -> p (g n)"),
                in_=grouped[x, q][:, s].rearrange("p g n t -> p (g n t)"),
            )

        weights = ((gcn_words, gcn_planes), (proj_words, proj_planes))

        def multiply(product, b, x):
            w_words, w_planes = weights[x]
            for g in range(PASSES):
                nc.tensor.matmul_mx(
                    out=product,
                    lhsT=words[x, b // 2][:, b % 2, g].bitcast(FP8X4),
                    lhsT_scale=planes[x, b // 2][:, b % 2, g],
                    rhs=w_words[:, g, :].bitcast(FP4X4),
                    rhs_scale=w_planes[:, g, :],
                    start=(g == 0),
                    stop=(g == PASSES - 1),
                )

        def repeat_pass(n):
            bank = bank_tile([P, OUT_FEATURES], F32, "agg")
            for i in range(n):
                nc.tensor.matmul_mx(
                    out=bank[:],
                    lhsT=words[GCN, 0][:, 0, 0].bitcast(FP8X4),
                    lhsT_scale=planes[GCN, 0][:, 0, 0],
                    rhs=gcn_words[:, 0, :].bitcast(FP4X4),
                    rhs_scale=gcn_planes[:, 0, :],
                    start=True,
                    stop=True,
                )

        def product_tile(shape, tag="product"):
            return bank_tile(shape, F32, tag)

        def scale(b, n, gcn_product):
            scaled = per_sample.tile([P, n, OUT_FEATURES], F32, name="scaled")
            nc.vector.tensor_tensor(out=scaled[:], in0=gcn_product, in1=spread[:, 1].to_broadcast([P, n, OUT_FEATURES]), op=MULT)
            return scaled

        def add_bias(b, n, scaled, engine):
            part = per_sample.tile([P, n, OUT_FEATURES], F32, name="part")
            engine.tensor_tensor(out=part[:], in0=scaled[:], in1=spread[:, 0].to_broadcast([P, n, OUT_FEATURES]), op=ADD)
            return part

        def finish(b, n, att_product, part):
            result = per_sample.tile([P, n, OUT_FEATURES], F32, name="result")
            nc.vector.tensor_tensor(out=result[:], in0=att_product, in1=part, op=ADD)
            nc.sync.dma_start(out=out[b : b + n].rearrange("b n f -> n b f"), in_=result[:])

        scalar_copy, vector_copy = nc.scalar.copy, nc.vector.tensor_copy
        aggregate(0, 0, vector_copy)
        aggregate(0, 1, scalar_copy)
        aggregate(1, 0, vector_copy)
        aggregate(1, 1, scalar_copy)
        aggregate(2, 0, scalar_copy)
        aggregate(2, 1, scalar_copy)
        quantise_pair(GCN, 0)
        spread_bank = bank_tile([P, 2, OUT_FEATURES], F32, "product")
        nc.tensor.matmul(out=spread_bank[:], lhsT=ones[:], rhs=vector_rows[:], start=True, stop=True)
        nc.vector.tensor_copy(out=spread[:, :, 0], in_=spread_bank[:])
        aggregate(3, 0, vector_copy)
        aggregate(3, 1, scalar_copy)
        transpose_attention(0, 0, PASSES, scalar_copy)
        gcn01 = product_tile([P, 2, OUT_FEATURES])
        multiply(gcn01[:, 0, :], 0, GCN)
        multiply(gcn01[:, 1, :], 1, GCN)
        scaled01 = scale(0, 2, gcn01[:])
        repeat_pass(5)
        quantise_pair(GCN, 1)
        transpose_attention(1, 0, PASSES, scalar_copy)
        part01 = add_bias(0, 2, scaled01, nc.vector)
        quantise(ATT, 0)
        transpose_attention(2, 0, PASSES, scalar_copy)
        gcn23 = product_tile([P, 2, OUT_FEATURES])
        multiply(gcn23[:, 0, :], 2, GCN)
        multiply(gcn23[:, 1, :], 3, GCN)
        quantise(ATT, 1)
        scaled23 = scale(2, 2, gcn23[:])
        quantise(ATT, 2)
        transpose_attention(3, 0, PASSES, scalar_copy)
        att01 = product_tile([P, 2, OUT_FEATURES])
        multiply(att01[:, 0, :], 0, ATT)
        multiply(att01[:, 1, :], 1, ATT)
        repeat_pass(4)
        att2 = product_tile([P, 1, OUT_FEATURES])
        multiply(att2[:, 0, :], 2, ATT)
        part23 = add_bias(2, 2, scaled23, nc.vector)
        quantise(ATT, 3)
        finish(0, 2, att01[:], part01[:])
        att3 = product_tile([P, 1, OUT_FEATURES], "agg")
        multiply(att3[:, 0, :], 3, ATT)
        finish(2, 1, att2[:], part23[:, 0:1])
        finish(3, 1, att3[:], part23[:, 1:2])
